import numpy as np
import ml_dtypes


def mxq(x, axis, fmt="e4m3"):
    dtype, down = {"e4m3": (ml_dtypes.float8_e4m3fn, 7), "e5m2": (ml_dtypes.float8_e5m2, 14)}[fmt]
    v = np.moveaxis(np.asarray(x, np.float32).astype(ml_dtypes.bfloat16).astype(np.float64), axis, -1)
    blocks = v.reshape(v.shape[:-1] + (-1, 32))
    amax = np.abs(blocks).max(-1, keepdims=True)
    byte = np.maximum(np.where(amax > 0, np.frexp(amax)[1] - 1 + 127, 0) - down, 1)
    scale = np.exp2(byte - 127.0)
    codes = (blocks / scale).astype(np.float32).astype(dtype).astype(np.float64)
    return np.moveaxis((codes * scale).reshape(v.shape), -1, axis)


WIDE = False


def mx_kscale(k):
    if not WIDE:
        return np.ones(k)
    levels = np.array([10, -10, 5, -5, 0])
    if k % 512:
        return np.exp2(np.random.permutation(np.resize(levels, k // 32))).repeat(32)
    a = np.empty((k // 512, 16))
    for p in range(k // 512):
        a[p, :8] = np.random.permutation(np.resize(levels, 8))
        for g in range(8):
            far = levels[np.abs(levels - a[p, g]) >= 10]
            a[p, g + 8] = far[np.random.randint(len(far))]
    return np.exp2(a.ravel()).repeat(32)


BF16 = ml_dtypes.bfloat16


def bf(x):
    return np.asarray(x, np.float32).astype(BF16)


def f64(x):
    return np.asarray(x).astype(np.float64)


B, N, D = 512, 17, 512
LN_EPS = 1e-5
LEAKY_SLOPE = 0.01


def setup_inputs():
    s = mx_kscale(D)
    s = s / s.max()
    return {"h": bf(np.random.standard_normal((B, N, D)) * 0.5 * s),
            "W_l": bf(np.random.standard_normal((D, D)) * 2.0 / np.sqrt(D) / s[None, :]),
            "b_l": bf(np.random.standard_normal(D) * 0.1),
            "W_r": bf(np.random.standard_normal((D, D)) * 1.0 / np.sqrt(D) / s[None, :]),
            "ln_g": bf(1.0 + 0.1 * np.random.standard_normal(D)),
            "ln_b": bf(-0.4 + 0.2 * np.random.standard_normal(D))}


def reference(h, W_l, b_l, W_r, ln_g, ln_b):
    h = f64(h)
    n = h.shape[1]
    mean_neigh = (np.sum(h, axis=1, keepdims=True) - h) / (n - 1)
    c = ((mxq(mean_neigh, 2, "e4m3") @ mxq(f64(W_l), 1, "e4m3").T) + f64(b_l)
         + (mxq(h, 2, "e4m3") @ mxq(f64(W_r), 1, "e4m3").T))
    mu = np.mean(c, axis=-1, keepdims=True)
    var = np.mean(np.square(c - mu), axis=-1, keepdims=True)
    y = (c - mu) * (1.0 / np.sqrt(var + LN_EPS)) * f64(ln_g) + f64(ln_b)
    a = np.where(y > 0, y, LEAKY_SLOPE * y)
    return a + h

@@ -1,0 +1,408 @@
+from contextlib import ExitStack
+
+import concourse.mybir as mybir
+from concourse.masks import make_identity
+
+F32 = mybir.dt.float32
+BF16 = mybir.dt.bfloat16
+I32 = mybir.dt.int32
+U32 = mybir.dt.uint32
+U8 = mybir.dt.uint8
+FP8X4 = mybir.dt.float8_e4m3fn_x4
+ALU = mybir.AluOpType
+ACT = mybir.ActivationFunctionType
+AXIS = mybir.AxisListType
+
+P = 128
+PACK = 4
+HALVES = 2
+GRAPHS = 512
+NODES = 17
+D = 512
+CHUNKS = D // P
+BLOCKS = GRAPHS // P
+OTHERS = NODES - 1
+LAST = NODES - 1
+GRAPHS_PER_SUM = P // OTHERS
+SUMS = P // GRAPHS_PER_SUM
+LN_EPS = 1e-5
+LEAKY_SLOPE = 0.01
+PAIR = 2
+SUMS_PER_STEP = 4
+LOADS_PER_STEP = 2
+DEPTH = 9
+
+FLOPS = 2 * 2 * GRAPHS * NODES * D * D
+
+
+def turn_words(nc, identity, rows, turned):
+    words = rows.bitcast(F32)
+    for u in range(HALVES):
+        nc.tensor.transpose(turned[:, u, :], words[:, u::HALVES], identity[:])
+
+
+def group_words(nc, turned, grouped):
+    nc.scalar.copy(out=grouped.bitcast(F32), in_=turned[:].rearrange("p j u r -> p j r u"))
+
+
+def quantise_weight(nc, stage, turned_pool, identity, weight, codes, scales):
+    rows = stage.tile([P, CHUNKS, D], BF16, name="weight_rows")
+    nc.sync.dma_start(out=rows[:], in_=weight.rearrange("(a p) k -> p a k", p=P))
+    grouped = stage.tile([P, D, PACK], BF16, name="weight_grouped", align_bytes=64)
+    for a in range(0, CHUNKS, PAIR):
+        turned = turned_pool.tile([P, PAIR, HALVES, P], F32)
+        for j in range(PAIR):
+            turn_words(nc, identity, rows[:, a + j, :], turned[:, j, :, :])
+        group_words(
+            nc, turned, grouped[:, a * P : (a + PAIR) * P, :].rearrange("p (j o) t -> p j o t", j=PAIR)
+        )
+    nc.vector.quantize_mx(
+        out=codes[:].bitcast(FP8X4),
+        scales=scales[:],
+        in_=grouped[:].rearrange("p o t -> p (o t)"),
+    )
+
+
+def tile_gnnnicheencoder_pa_t_kernel(tc, h, W_l, b_l, W_r, ln_g, ln_b, out):
+    nc = tc.nc
+    with ExitStack() as stack:
+        stack.enter_context(tc.manual_schedule())
+        const = stack.enter_context(tc.tile_pool(name="const", bufs=1))
+        stage = stack.enter_context(tc.tile_pool(name="stage", bufs=2))
+        blocks = stack.enter_context(tc.tile_pool(name="blocks", bufs=BLOCKS))
+        means = stack.enter_context(tc.tile_pool(name="means", bufs=2))
+        work = stack.enter_context(tc.tile_pool(name="work", bufs=2))
+        stats = stack.enter_context(tc.tile_pool(name="stats", bufs=4))
+        turned_pool = stack.enter_context(tc.psum_pool(name="turned", bufs=1))
+        sums_pool = stack.enter_context(tc.psum_pool(name="sums", bufs=1))
+        acc_pool = stack.enter_context(tc.psum_pool(name="acc", bufs=PAIR))
+        features_pool = stack.enter_context(tc.psum_pool(name="features", bufs=PAIR))
+        rows_pool = stack.enter_context(tc.psum_pool(name="rows", bufs=PAIR))
+
+        identity = const.tile([P, P], F32)
+        make_identity(nc, identity[:])
+        graph_of_partition = const.tile([P, GRAPHS_PER_SUM], F32)
+        nc.vector.tensor_reduce(
+            out=graph_of_partition[:],
+            in_=identity[:].rearrange("p (i g) -> p g i", g=GRAPHS_PER_SUM),
+            axis=AXIS.X,
+            op=ALU.add,
+        )
+        node_sum = const.tile([P, GRAPHS_PER_SUM], BF16)
+        nc.vector.tensor_scalar_mul(out=node_sum[:], in0=graph_of_partition[:], scalar1=1.0 / OTHERS)
+        sixteenth = const.tile([P, P], BF16)
+        nc.vector.tensor_scalar_mul(out=sixteenth[:], in0=identity[:], scalar1=1.0 / OTHERS)
+        eps = const.tile([P, 1], F32)
+        nc.vector.memset(eps[:], LN_EPS)
+        vector_rows = const.tile([P, P], BF16)
+        nc.vector.memset(vector_rows[:].bitcast(I32), 0)
+
+        wr_codes = const.tile([P, D], U32, align_bytes=64)
+        wr_scales = const.tile([P, D], U8, align_bytes=64)
+        wl_codes = const.tile([P, D], U32, align_bytes=64)
+        wl_scales = const.tile([P, D], U8, align_bytes=64)
+        quantise_weight(nc, stage, turned_pool, identity, W_r, wr_codes, wr_scales)
+        quantise_weight(nc, stage, turned_pool, identity, W_l, wl_codes, wl_scales)
+
+        by_graph = {}
+        by_node = {}
+
+        def load_graphs(s):
+            block = h[s * P : (s + 1) * P, :, :]
+            by_graph[s] = blocks.tile([P, NODES, D], BF16, name="by_graph")
+            nc.sync.dma_start(out=by_graph[s][:, LAST, :], in_=block[:, LAST, :])
+            nc.sync.dma_start(out=by_graph[s][:, 0:LAST, :], in_=block[:, 0:LAST, :])
+
+        def load_nodes(s, g):
+            if g == 0:
+                by_node[s] = blocks.tile([P, SUMS, D], BF16, name="by_node", bufs=2)
+            spread = h[s * P : (s + 1) * P, 0:LAST, :].rearrange(
+                "(T g) i k -> g i T k", g=GRAPHS_PER_SUM
+            )
+            nc.sync.dma_start(out=by_node[s][g:P:GRAPHS_PER_SUM, :, :], in_=spread[g])
+
+        load_graphs(0)
+        bias_rows = const.tile([P, D], BF16)
+        nc.sync.dma_start(out=bias_rows[:], in_=b_l.partition_broadcast(P))
+        nc.sync.dma_start(out=vector_rows[0:CHUNKS, :], in_=ln_g.rearrange("(f p) -> f p", p=P))
+        nc.sync.dma_start(
+            out=vector_rows[CHUNKS : 2 * CHUNKS, :], in_=ln_b.rearrange("(f p) -> f p", p=P)
+        )
+
+        tiles = [(s, i) for s in range(BLOCKS) for i in [LAST] + list(range(LAST))]
+        count = len(tiles) // PAIR
+        pair_of_last = [s * NODES // PAIR for s in range(BLOCKS)]
+        sums_of = {}
+        mean_of = {}
+        kept = {}
+
+        def sum_nodes(s, T):
+            if T == 0:
+                sums_of[s] = sums_pool.tile([P, PACK, P], F32, name="sums")
+            columns = by_node[s][:, T, :].rearrange("p (q t) -> p t q", t=PACK)
+            for t in range(PACK):
+                nc.tensor.matmul(
+                    out=sums_of[s][:, t, T * GRAPHS_PER_SUM : (T + 1) * GRAPHS_PER_SUM],
+                    lhsT=columns[:, t, :],
+                    rhs=node_sum[:],
+                    start=True,
+                    stop=True,
+                )
+
+        def sum_nodes_of_first_block():
+            sums_of[0] = sums_pool.tile([P, PACK, P], F32, name="sums")
+            for t in range(PACK):
+                for i in range(LAST):
+                    columns = by_graph[0][:, i, :].rearrange("p (q t) -> p t q", t=PACK)
+                    nc.tensor.matmul(
+                        out=sums_of[0][:, t, :],
+                        lhsT=columns[:, t, :],
+                        rhs=sixteenth[:],
+                        start=(i == 0),
+                        stop=(i == LAST - 1),
+                    )
+
+        def turn(q):
+            turned = turned_pool.tile([P, PAIR, HALVES, P], F32)
+            for j in range(PAIR):
+                s, i = tiles[PAIR * q + j]
+                turn_words(nc, identity, by_graph[s][:, i, :], turned[:, j, :, :])
+            kept[("turned", q)] = turned
+
+        def group(q):
+            grouped = work.tile([P, 2, PAIR, P, PACK], BF16, name="grouped", align_bytes=64, bufs=3)
+            group_words(nc, kept[("turned", q)], grouped[:, 0, :, :, :])
+            kept[("grouped", q)] = grouped
+
+        def neighbours(q):
+            grouped = kept[("grouped", q)]
+            for j in range(PAIR):
+                s, i = tiles[PAIR * q + j]
+                if i == LAST:
+                    mean = means.tile([P, P, PACK], F32, name="mean")
+                    nc.vector.scalar_tensor_tensor(
+                        out=mean[:],
+                        in0=grouped[:, 0, j, :, :],
+                        scalar=1.0 / OTHERS,
+                        in1=sums_of[s][:].rearrange("p t g -> p g t"),
+                        op0=ALU.mult,
+                        op1=ALU.add,
+                    )
+                    mean_of[s] = mean
+                nc.vector.scalar_tensor_tensor(
+                    out=grouped[:, 1, j, :, :],
+                    in0=grouped[:, 0, j, :, :],
+                    scalar=-1.0 / OTHERS,
+                    in1=mean_of[s][:],
+                    op0=ALU.mult,
+                    op1=ALU.add,
+                )
+
+        def quantise(q):
+            codes = work.tile([P, 2, PAIR, P], U32, name="codes", align_bytes=64)
+            scales = work.tile([P, 2, PAIR, P], U8, name="scales", align_bytes=64)
+            nc.vector.quantize_mx(
+                out=codes[:].rearrange("p x j r -> p (x j r)").bitcast(FP8X4),
+                scales=scales[:].rearrange("p x j r -> p (x j r)"),
+                in_=kept[("grouped", q)][:].rearrange("p x j r t -> p (x j r t)"),
+            )
+            kept[("codes", q)] = (codes, scales)
+
+        def multiply(q):
+            codes, scales = kept[("codes", q)]
+            banks = []
+            for j in range(PAIR):
+                acc = acc_pool.tile([P, D], F32)
+                nc.tensor.matmul_mx(
+                    out=acc[:],
+                    lhsT=codes[:, 0, j, :].bitcast(FP8X4),
+                    lhsT_scale=scales[:, 0, j, :],
+                    rhs=wr_codes[:].bitcast(FP8X4),
+                    rhs_scale=wr_scales[:],
+                    start=True,
+                    stop=False,
+                )
+                nc.tensor.matmul_mx(
+                    out=acc[:],
+                    lhsT=codes[:, 1, j, :].bitcast(FP8X4),
+                    lhsT_scale=scales[:, 1, j, :],
+                    rhs=wl_codes[:].bitcast(FP8X4),
+                    rhs_scale=wl_scales[:],
+                    start=False,
+                    stop=True,
+                )
+                banks.append(acc)
+            kept[("acc", q)] = banks
+
+        def add_bias(q):
+            c = work.tile([P, PAIR, D], F32, name="c", bufs=3)
+            row_sum = stats.tile([P, PAIR], F32, name="row_sum")
+            for j in range(PAIR):
+                nc.vector.scalar_tensor_tensor(
+                    out=c[:, j, :],
+                    in0=kept[("acc", q)][j][:],
+                    scalar=1.0,
+                    in1=bias_rows[:],
+                    op0=ALU.mult,
+                    op1=ALU.add,
+                    accum_out=row_sum[:, j : j + 1],
+                )
+            kept[("c", q)] = c
+            kept[("row_sum", q)] = row_sum
+
+        def negate_mean(q):
+            minus_mean = stats.tile([P, PAIR], F32, name="minus_mean")
+            nc.scalar.mul(out=minus_mean[:], in_=kept[("row_sum", q)][:], mul=-1.0 / D)
+            kept[("minus_mean", q)] = minus_mean
+
+        def sum_squares(q):
+            square_sum = stats.tile([P, PAIR], F32, name="square_sum")
+            for j in range(PAIR):
+                squares = work.tile([P, D], BF16, name="squares")
+                nc.scalar.activation(
+                    out=squares[:],
+                    in_=kept[("c", q)][:, j, :],
+                    func=ACT.Square,
+                    bias=kept[("minus_mean", q)][:, j : j + 1],
+                    scale=1.0,
+                    accum_out=square_sum[:, j : j + 1],
+                )
+            kept[("square_sum", q)] = square_sum
+
+        def invert_deviation(q):
+            inverse = stats.tile([P, PAIR], F32, name="inverse")
+            nc.scalar.activation(
+                out=inverse[:],
+                in_=kept[("square_sum", q)][:],
+                func=ACT.Abs_reciprocal_sqrt,
+                bias=eps[:],
+                scale=1.0 / D,
+            )
+            kept[("inverse", q)] = inverse
+
+        def normalise(q):
+            normal = work.tile([P, PAIR, D], F32, name="normal")
+            for j in range(PAIR):
+                nc.gpsimd.tensor_scalar(
+                    out=normal[:, j, :],
+                    in0=kept[("c", q)][:, j, :],
+                    scalar1=kept[("minus_mean", q)][:, j : j + 1],
+                    scalar2=kept[("inverse", q)][:, j : j + 1],
+                    op0=ALU.add,
+                    op1=ALU.mult,
+                )
+            kept[("normal", q)] = normal
+
+        def to_features(q):
+            normal = kept[("normal", q)]
+            banks = []
+            for half in range(CHUNKS // 2):
+                normal_turned = features_pool.tile([P, 2, PAIR, P], F32)
+                for x in range(2):
+                    f = 2 * half + x
+                    for j in range(PAIR):
+                        nc.tensor.transpose(
+                            normal_turned[:, x, j, :], normal[:, j, f * P : (f + 1) * P], identity[:]
+                        )
+                banks.append(normal_turned)
+            kept[("normal_turned", q)] = banks
+
+        def two_terms(q):
+            bent = work.tile([P, CHUNKS, PAIR, P], F32, name="bent")
+            straight = work.tile([P, CHUNKS, PAIR, P], F32, name="straight")
+            for f in range(CHUNKS):
+                normal_turned = kept[("normal_turned", q)][f // 2][:, f % 2, :, :]
+                nc.scalar.activation(
+                    out=bent[:, f, :, :],
+                    in_=normal_turned,
+                    func=ACT.Relu,
+                    bias=relu_term[:, CHUNKS + f : CHUNKS + f + 1],
+                    scale=relu_term[:, f : f + 1],
+                )
+                nc.scalar.activation(
+                    out=straight[:, f, :, :],
+                    in_=normal_turned,
+                    func=ACT.Identity,
+                    bias=line_term[:, CHUNKS + f : CHUNKS + f + 1],
+                    scale=line_term[:, f : f + 1],
+                )
+            kept[("terms", q)] = (bent, straight)
+
+        def to_rows(q):
+            bent, straight = kept[("terms", q)]
+            banks = []
+            for j in range(PAIR):
+                a_rows = rows_pool.tile([P, D], F32)
+                for f in range(CHUNKS):
+                    nc.tensor.matmul(
+                        out=a_rows[:, f * P : (f + 1) * P],
+                        lhsT=bent[:, f, j, :],
+                        rhs=identity[:],
+                        is_transpose=True,
+                        start=True,
+                        stop=False,
+                    )
+                    nc.tensor.matmul(
+                        out=a_rows[:, f * P : (f + 1) * P],
+                        lhsT=straight[:, f, j, :],
+                        rhs=identity[:],
+                        is_transpose=True,
+                        start=False,
+                        stop=True,
+                    )
+                banks.append(a_rows)
+            kept[("a_rows", q)] = banks
+
+        def add_residual(q):
+            for j in range(PAIR):
+                s, i = tiles[PAIR * q + j]
+                result = work.tile([P, D], F32, name="result", bufs=4)
+                nc.vector.tensor_add(
+                    out=result[:], in0=kept[("a_rows", q)][j][:], in1=by_graph[s][:, i, :]
+                )
+                nc.sync.dma_start(out=out[s * P : (s + 1) * P, i, :], in_=result[:])
+
+        def run(stage_of_pair, q):
+            if 0 <= q < count:
+                stage_of_pair(q)
+
+        sum_nodes_of_first_block()
+
+        vector_rows_f32 = const.tile([P, P], F32)
+        nc.vector.tensor_copy(out=vector_rows_f32[:], in_=vector_rows[:])
+        turned = turned_pool.tile([P, PAIR, HALVES, P], F32)
+        nc.tensor.transpose(turned[:, 0, 0, :], vector_rows_f32[:], identity[:])
+        per_feature = const.tile([P, 2 * CHUNKS], F32)
+        nc.vector.tensor_copy(out=per_feature[:], in_=turned[:, 0, 0, 0 : 2 * CHUNKS])
+        relu_term = const.tile([P, 2 * CHUNKS], F32)
+        nc.vector.tensor_scalar_mul(out=relu_term[:], in0=per_feature[:], scalar1=1.0 - LEAKY_SLOPE)
+        line_term = const.tile([P, 2 * CHUNKS], F32)
+        nc.vector.tensor_scalar_mul(out=line_term[:], in0=per_feature[:], scalar1=LEAKY_SLOPE)
+
+        for k in range(count + DEPTH):
+            for s in range(1, BLOCKS):
+                since = k - pair_of_last[s - 1]
+                if 0 <= since < GRAPHS_PER_SUM // LOADS_PER_STEP:
+                    for g in range(LOADS_PER_STEP * since, LOADS_PER_STEP * (since + 1)):
+                        load_nodes(s, g)
+                if since == GRAPHS_PER_SUM // LOADS_PER_STEP:
+                    load_graphs(s)
+            run(add_residual, k - 9)
+            run(add_bias, k - 4)
+            run(normalise, k - 6)
+            run(negate_mean, k - 5)
+            run(group, k - 1)
+            run(to_features, k - 7)
+            run(to_rows, k - 8)
+            run(turn, k)
+            for s in range(1, BLOCKS):
+                first = pair_of_last[s] + 1 - SUMS // SUMS_PER_STEP
+                if first <= k < first + SUMS // SUMS_PER_STEP:
+                    for T in range(SUMS_PER_STEP * (k - first), SUMS_PER_STEP * (k - first + 1)):
+                        sum_nodes(s, T)
+            run(multiply, k - 3)
+            run(sum_squares, k - 5)
+            run(two_terms, k - 7)
+            run(invert_deviation, k - 5)
+            run(quantise, k - 2)
+            run(neighbours, k - 1)

@@ -30,6 +30,8 @@ LEAKY_SLOPE = 0.01
 PAIR = 2
 SUMS_PER_STEP = 4
 LOADS_PER_STEP = 2
+NODES_PER_LOAD = 4
+HEAD = 2
 DEPTH = 9
 
 FLOPS = 2 * 2 * GRAPHS * NODES * D * D
@@ -45,17 +47,25 @@ def group_words(nc, turned, grouped):
     nc.scalar.copy(out=grouped.bitcast(F32), in_=turned[:].rearrange("p j u r -> p j r u"))
 
 
-def quantise_weight(nc, stage, turned_pool, identity, weight, codes, scales):
+def load_weight(nc, stage, weight):
     rows = stage.tile([P, CHUNKS, D], BF16, name="weight_rows")
     nc.sync.dma_start(out=rows[:], in_=weight.rearrange("(a p) k -> p a k", p=P))
+    return rows
+
+
+def turn_weight(nc, stage, turned_pool, identity, rows):
     grouped = stage.tile([P, D, PACK], BF16, name="weight_grouped", align_bytes=64)
     for a in range(0, CHUNKS, PAIR):
-        turned = turned_pool.tile([P, PAIR, HALVES, P], F32)
+        turned = turned_pool.tile([P, PAIR, HALVES, P], F32, name="normal_turned")
         for j in range(PAIR):
             turn_words(nc, identity, rows[:, a + j, :], turned[:, j, :, :])
         group_words(
             nc, turned, grouped[:, a * P : (a + PAIR) * P, :].rearrange("p (j o) t -> p j o t", j=PAIR)
         )
+    return grouped
+
+
+def quantise_weight(nc, grouped, codes, scales):
     nc.vector.quantize_mx(
         out=codes[:].bitcast(FP8X4),
         scales=scales[:],
@@ -101,8 +111,6 @@ def tile_gnnnicheencoder_pa_t_kernel(tc, h, W_l, b_l, W_r, ln_g, ln_b, out):
         wr_scales = const.tile([P, D], U8, align_bytes=64)
         wl_codes = const.tile([P, D], U32, align_bytes=64)
         wl_scales = const.tile([P, D], U8, align_bytes=64)
-        quantise_weight(nc, stage, turned_pool, identity, W_r, wr_codes, wr_scales)
-        quantise_weight(nc, stage, turned_pool, identity, W_l, wl_codes, wl_scales)
 
         by_graph = {}
         by_node = {}
@@ -111,7 +119,11 @@ def tile_gnnnicheencoder_pa_t_kernel(tc, h, W_l, b_l, W_r, ln_g, ln_b, out):
             block = h[s * P : (s + 1) * P, :, :]
             by_graph[s] = blocks.tile([P, NODES, D], BF16, name="by_graph")
             nc.sync.dma_start(out=by_graph[s][:, LAST, :], in_=block[:, LAST, :])
-            nc.sync.dma_start(out=by_graph[s][:, 0:LAST, :], in_=block[:, 0:LAST, :])
+            at_once = NODES_PER_LOAD if s == 0 else LAST
+            for i in range(0, LAST, at_once):
+                nc.sync.dma_start(
+                    out=by_graph[s][:, i : i + at_once, :], in_=block[:, i : i + at_once, :]
+                )
 
         def load_nodes(s, g):
             if g == 0:
@@ -122,6 +134,8 @@ def tile_gnnnicheencoder_pa_t_kernel(tc, h, W_l, b_l, W_r, ln_g, ln_b, out):
             nc.sync.dma_start(out=by_node[s][g:P:GRAPHS_PER_SUM, :, :], in_=spread[g])
 
         load_graphs(0)
+        wr_rows = load_weight(nc, stage, W_r)
+        wl_rows = load_weight(nc, stage, W_l)
         bias_rows = const.tile([P, D], BF16)
         nc.sync.dma_start(out=bias_rows[:], in_=b_l.partition_broadcast(P))
         nc.sync.dma_start(out=vector_rows[0:CHUNKS, :], in_=ln_g.rearrange("(f p) -> f p", p=P))
@@ -149,18 +163,23 @@ def tile_gnnnicheencoder_pa_t_kernel(tc, h, W_l, b_l, W_r, ln_g, ln_b, out):
                     stop=True,
                 )
 
-        def sum_nodes_of_first_block():
-            sums_of[0] = sums_pool.tile([P, PACK, P], F32, name="sums")
+        def add_nodes(row_sums, nodes):
+            for i in nodes:
+                nc.tensor.matmul(
+                    out=row_sums[:],
+                    lhsT=sixteenth[:],
+                    rhs=by_graph[0][:, i, :],
+                    start=(i == LAST),
+                    stop=(i == LAST - 1),
+                )
+
+        def turn_mean(mean_rows):
+            mean_turned = sums_pool.tile([P, PACK, P], F32, name="sums")
             for t in range(PACK):
-                for i in range(LAST):
-                    columns = by_graph[0][:, i, :].rearrange("p (q t) -> p t q", t=PACK)
-                    nc.tensor.matmul(
-                        out=sums_of[0][:, t, :],
-                        lhsT=columns[:, t, :],
-                        rhs=sixteenth[:],
-                        start=(i == 0),
-                        stop=(i == LAST - 1),
-                    )
+                nc.tensor.transpose(mean_turned[:, t, :], mean_rows[:, t::PACK], identity[:])
+            mean = means.tile([P, P, PACK], F32, name="mean")
+            nc.scalar.copy(out=mean[:], in_=mean_turned[:].rearrange("p t g -> p g t"))
+            mean_of[0] = mean
 
         def turn(q):
             turned = turned_pool.tile([P, PAIR, HALVES, P], F32)
@@ -178,7 +197,7 @@ def tile_gnnnicheencoder_pa_t_kernel(tc, h, W_l, b_l, W_r, ln_g, ln_b, out):
             grouped = kept[("grouped", q)]
             for j in range(PAIR):
                 s, i = tiles[PAIR * q + j]
-                if i == LAST:
+                if s not in mean_of:
                     mean = means.tile([P, P, PACK], F32, name="mean")
                     nc.vector.scalar_tensor_tensor(
                         out=mean[:],
@@ -362,26 +381,46 @@ def tile_gnnnicheencoder_pa_t_kernel(tc, h, W_l, b_l, W_r, ln_g, ln_b, out):
                 )
                 nc.sync.dma_start(out=out[s * P : (s + 1) * P, i, :], in_=result[:])
 
+        def spread_vectors():
+            vector_rows_f32 = const.tile([P, P], F32)
+            nc.vector.tensor_copy(out=vector_rows_f32[:], in_=vector_rows[:])
+            vectors_turned = features_pool.tile([P, P], F32, name="normal_turned")
+            nc.tensor.transpose(vectors_turned[:], vector_rows_f32[:], identity[:])
+            per_feature = const.tile([P, 2 * CHUNKS], F32)
+            nc.vector.tensor_copy(out=per_feature[:], in_=vectors_turned[:, 0 : 2 * CHUNKS])
+            relu_term = const.tile([P, 2 * CHUNKS], F32)
+            nc.vector.tensor_scalar_mul(out=relu_term[:], in0=per_feature[:], scalar1=1.0 - LEAKY_SLOPE)
+            line_term = const.tile([P, 2 * CHUNKS], F32)
+            nc.vector.tensor_scalar_mul(out=line_term[:], in0=per_feature[:], scalar1=LEAKY_SLOPE)
+            return relu_term, line_term
+
         def run(stage_of_pair, q):
             if 0 <= q < count:
                 stage_of_pair(q)
 
-        sum_nodes_of_first_block()
+        row_sums = sums_pool.tile([P, D], F32, name="sums")
+        turn(0)
+        group(0)
+        add_nodes(row_sums, [LAST, *range(NODES_PER_LOAD)])
+        turn(1)
+        group(1)
+        add_nodes(row_sums, range(NODES_PER_LOAD, LAST))
+        mean_rows = means.tile([P, D], F32, name="mean_rows", bufs=1)
+        nc.scalar.copy(out=mean_rows[:], in_=row_sums[:])
+        wr_grouped = turn_weight(nc, stage, features_pool, identity, wr_rows)
+        turn_mean(mean_rows)
+        quantise_weight(nc, wr_grouped, wr_codes, wr_scales)
+        neighbours(0)
+        wl_grouped = turn_weight(nc, stage, features_pool, identity, wl_rows)
+        quantise(0)
+        neighbours(1)
+        quantise_weight(nc, wl_grouped, wl_codes, wl_scales)
 
-        vector_rows_f32 = const.tile([P, P], F32)
-        nc.vector.tensor_copy(out=vector_rows_f32[:], in_=vector_rows[:])
-        turned = turned_pool.tile([P, PAIR, HALVES, P], F32)
-        nc.tensor.transpose(turned[:, 0, 0, :], vector_rows_f32[:], identity[:])
-        per_feature = const.tile([P, 2 * CHUNKS], F32)
-        nc.vector.tensor_copy(out=per_feature[:], in_=turned[:, 0, 0, 0 : 2 * CHUNKS])
-        relu_term = const.tile([P, 2 * CHUNKS], F32)
-        nc.vector.tensor_scalar_mul(out=relu_term[:], in0=per_feature[:], scalar1=1.0 - LEAKY_SLOPE)
-        line_term = const.tile([P, 2 * CHUNKS], F32)
-        nc.vector.tensor_scalar_mul(out=line_term[:], in0=per_feature[:], scalar1=LEAKY_SLOPE)
-
-        for k in range(count + DEPTH):
+        for k in range(HEAD, count + DEPTH):
+            if k == 4:
+                relu_term, line_term = spread_vectors()
             for s in range(1, BLOCKS):
-                since = k - pair_of_last[s - 1]
+                since = k - max(pair_of_last[s - 1], HEAD)
                 if 0 <= since < GRAPHS_PER_SUM // LOADS_PER_STEP:
                     for g in range(LOADS_PER_STEP * since, LOADS_PER_STEP * (since + 1)):
                         load_nodes(s, g)
@@ -391,7 +430,8 @@ def tile_gnnnicheencoder_pa_t_kernel(tc, h, W_l, b_l, W_r, ln_g, ln_b, out):
             run(add_bias, k - 4)
             run(normalise, k - 6)
             run(negate_mean, k - 5)
-            run(group, k - 1)
+            if k > HEAD:
+                run(group, k - 1)
             run(to_features, k - 7)
             run(to_rows, k - 8)
             run(turn, k)
@@ -404,5 +444,6 @@ def tile_gnnnicheencoder_pa_t_kernel(tc, h, W_l, b_l, W_r, ln_g, ln_b, out):
             run(sum_squares, k - 5)
             run(two_terms, k - 7)
             run(invert_deviation, k - 5)
-            run(quantise, k - 2)
-            run(neighbours, k - 1)
+            if k > HEAD:
+                run(quantise, k - 2)
+                run(neighbours, k - 1)

@@ -22,15 +22,14 @@ D = 512
 CHUNKS = D // P
 BLOCKS = GRAPHS // P
 OTHERS = NODES - 1
-LAST = NODES - 1
-GRAPHS_PER_SUM = P // OTHERS
-SUMS = P // GRAPHS_PER_SUM
+TOUCHED = 9
 LN_EPS = 1e-5
 LEAKY_SLOPE = 0.01
 PAIR = 2
-SUMS_PER_STEP = 4
-LOADS_PER_STEP = 2
-NODES_PER_LOAD = 4
+RUNS = [(0, 1), (1, 5), (5, 9), (9, 13), (13, 17)]
+LOAD_AHEAD = 1
+EARLY_PASSES = 12
+LATE_PASSES = 9
 HEAD = 2
 DEPTH = 9
 
@@ -80,7 +79,7 @@ def tile_gnnnicheencoder_pa_t_kernel(tc, h, W_l, b_l, W_r, ln_g, ln_b, out):
         const = stack.enter_context(tc.tile_pool(name="const", bufs=1))
         stage = stack.enter_context(tc.tile_pool(name="stage", bufs=2))
         blocks = stack.enter_context(tc.tile_pool(name="blocks", bufs=BLOCKS))
-        means = stack.enter_context(tc.tile_pool(name="means", bufs=2))
+        means = stack.enter_context(tc.tile_pool(name="means", bufs=BLOCKS))
         work = stack.enter_context(tc.tile_pool(name="work", bufs=2))
         stats = stack.enter_context(tc.tile_pool(name="stats", bufs=4))
         turned_pool = stack.enter_context(tc.psum_pool(name="turned", bufs=1))
@@ -91,15 +90,24 @@ def tile_gnnnicheencoder_pa_t_kernel(tc, h, W_l, b_l, W_r, ln_g, ln_b, out):
 
         identity = const.tile([P, P], F32)
         make_identity(nc, identity[:])
-        graph_of_partition = const.tile([P, GRAPHS_PER_SUM], F32)
-        nc.vector.tensor_reduce(
-            out=graph_of_partition[:],
-            in_=identity[:].rearrange("p (i g) -> p g i", g=GRAPHS_PER_SUM),
-            axis=AXIS.X,
-            op=ALU.add,
-        )
-        node_sum = const.tile([P, GRAPHS_PER_SUM], BF16)
-        nc.vector.tensor_scalar_mul(out=node_sum[:], in0=graph_of_partition[:], scalar1=1.0 / OTHERS)
+        diagonal = const.tile([P, NODES + TOUCHED * NODES], F32)
+        nc.vector.memset(diagonal[:], 0.0)
+        nc.vector.tensor_copy(out=diagonal[:, NODES : NODES + P], in_=identity[:])
+        graph_of_row = const.tile([P, NODES, TOUCHED], F32)
+        for T in range(NODES):
+            before = T * P % NODES
+            nc.vector.tensor_reduce(
+                out=graph_of_row[:, T, :],
+                in_=diagonal[:, NODES - before : NODES - before + TOUCHED * NODES].rearrange(
+                    "p (j i) -> p j i", i=NODES
+                ),
+                axis=AXIS.X,
+                op=ALU.add,
+            )
+        graph_sum = const.tile([P, NODES, TOUCHED], BF16)
+        nc.vector.tensor_scalar_mul(out=graph_sum[:], in0=graph_of_row[:], scalar1=1.0 / OTHERS)
+        nothing = const.tile([P, P], BF16)
+        nc.vector.memset(nothing[:].bitcast(I32), 0)
         sixteenth = const.tile([P, P], BF16)
         nc.vector.tensor_scalar_mul(out=sixteenth[:], in0=identity[:], scalar1=1.0 / OTHERS)
         eps = const.tile([P, 1], F32)
@@ -113,27 +121,24 @@ def tile_gnnnicheencoder_pa_t_kernel(tc, h, W_l, b_l, W_r, ln_g, ln_b, out):
         wl_scales = const.tile([P, D], U8, align_bytes=64)
 
         by_graph = {}
-        by_node = {}
+        by_row = {}
 
-        def load_graphs(s):
-            block = h[s * P : (s + 1) * P, :, :]
-            by_graph[s] = blocks.tile([P, NODES, D], BF16, name="by_graph")
-            nc.sync.dma_start(out=by_graph[s][:, LAST, :], in_=block[:, LAST, :])
-            at_once = NODES_PER_LOAD if s == 0 else LAST
-            for i in range(0, LAST, at_once):
-                nc.sync.dma_start(
-                    out=by_graph[s][:, i : i + at_once, :], in_=block[:, i : i + at_once, :]
-                )
-
-        def load_nodes(s, g):
-            if g == 0:
-                by_node[s] = blocks.tile([P, SUMS, D], BF16, name="by_node", bufs=2)
-            spread = h[s * P : (s + 1) * P, 0:LAST, :].rearrange(
-                "(T g) i k -> g i T k", g=GRAPHS_PER_SUM
+        def load_graphs(s, begin, end):
+            if begin == 0:
+                by_graph[s] = blocks.tile([P, NODES, D], BF16, name="by_graph")
+            nc.sync.dma_start(
+                out=by_graph[s][:, begin:end, :], in_=h[s * P : (s + 1) * P, begin:end, :]
             )
-            nc.sync.dma_start(out=by_node[s][g:P:GRAPHS_PER_SUM, :, :], in_=spread[g])
 
-        load_graphs(0)
+        def load_rows(s, begin, end):
+            if begin == 0:
+                by_row[s] = blocks.tile([P, NODES, D], BF16, name="by_row", bufs=BLOCKS - 1)
+            lines = h[s * P : (s + 1) * P, :, :].rearrange("g i k -> (g i) k")
+            lines = lines.rearrange("(T p) k -> p T k", p=P)
+            nc.sync.dma_start(out=by_row[s][:, begin:end, :], in_=lines[:, begin:end, :])
+
+        for run_of_nodes in RUNS:
+            load_graphs(0, *run_of_nodes)
         wr_rows = load_weight(nc, stage, W_r)
         wl_rows = load_weight(nc, stage, W_l)
         bias_rows = const.tile([P, D], BF16)
@@ -142,26 +147,54 @@ def tile_gnnnicheencoder_pa_t_kernel(tc, h, W_l, b_l, W_r, ln_g, ln_b, out):
         nc.sync.dma_start(
             out=vector_rows[CHUNKS : 2 * CHUNKS, :], in_=ln_b.rearrange("(f p) -> f p", p=P)
         )
+        for run_of_nodes in RUNS:
+            load_rows(1, *run_of_nodes)
+        for run_of_nodes in RUNS:
+            load_rows(2, *run_of_nodes)
+        for run_of_nodes in RUNS:
+            load_graphs(1, *run_of_nodes)
 
-        tiles = [(s, i) for s in range(BLOCKS) for i in [LAST] + list(range(LAST))]
+        tiles = [(s, i) for s in range(BLOCKS) for i in range(NODES)]
         count = len(tiles) // PAIR
-        pair_of_last = [s * NODES // PAIR for s in range(BLOCKS)]
+        first_pair = [s * NODES // PAIR for s in range(BLOCKS)]
         sums_of = {}
         mean_of = {}
         kept = {}
 
-        def sum_nodes(s, T):
-            if T == 0:
+        sum_passes = [(s, t, T) for s in range(1, BLOCKS) for t in range(PACK) for T in range(NODES)]
+        done_sums = []
+
+        def sum_nodes(k):
+            for x in range(EARLY_PASSES if k < DEPTH else LATE_PASSES):
+                if sum_passes:
+                    s, t, T = sum_passes.pop(0)
+                    sum_node(s, t, T)
+                    if (t, T) == (PACK - 1, NODES - 1):
+                        done_sums.append(s)
+                        if sum_passes:
+                            return
+
+        def sum_node(s, t, T):
+            if t == 0 and T == 0:
                 sums_of[s] = sums_pool.tile([P, PACK, P], F32, name="sums")
-            columns = by_node[s][:, T, :].rearrange("p (q t) -> p t q", t=PACK)
-            for t in range(PACK):
+            if T == 0:
                 nc.tensor.matmul(
-                    out=sums_of[s][:, t, T * GRAPHS_PER_SUM : (T + 1) * GRAPHS_PER_SUM],
-                    lhsT=columns[:, t, :],
-                    rhs=node_sum[:],
-                    start=True,
-                    stop=True,
+                    out=sums_of[s][:, t, :], lhsT=sixteenth[:], rhs=nothing[:], start=True, stop=False
                 )
+            begin = T * P // NODES
+            end = min(begin + TOUCHED, P)
+            nc.tensor.matmul(
+                out=sums_of[s][:, t, begin:end],
+                lhsT=by_row[s][:, T, :].rearrange("p (q t) -> p t q", t=PACK)[:, t, :],
+                rhs=graph_sum[:, T, 0 : end - begin],
+                start=False,
+                stop=(T == NODES - 1),
+            )
+
+        def keep_mean(s):
+            mean = means.tile([P, P, PACK], F32, name="mean")
+            nc.vector.tensor_copy(out=mean[:], in_=sums_of[s][:].rearrange("p t g -> p g t"))
+            mean_of[s] = mean
 
         def add_nodes(row_sums, nodes):
             for i in nodes:
@@ -169,8 +202,8 @@ def tile_gnnnicheencoder_pa_t_kernel(tc, h, W_l, b_l, W_r, ln_g, ln_b, out):
                     out=row_sums[:],
                     lhsT=sixteenth[:],
                     rhs=by_graph[0][:, i, :],
-                    start=(i == LAST),
-                    stop=(i == LAST - 1),
+                    start=(i == 0),
+                    stop=(i == NODES - 1),
                 )
 
         def turn_mean(mean_rows):
@@ -197,17 +230,6 @@ def tile_gnnnicheencoder_pa_t_kernel(tc, h, W_l, b_l, W_r, ln_g, ln_b, out):
             grouped = kept[("grouped", q)]
             for j in range(PAIR):
                 s, i = tiles[PAIR * q + j]
-                if s not in mean_of:
-                    mean = means.tile([P, P, PACK], F32, name="mean")
-                    nc.vector.scalar_tensor_tensor(
-                        out=mean[:],
-                        in0=grouped[:, 0, j, :, :],
-                        scalar=1.0 / OTHERS,
-                        in1=sums_of[s][:].rearrange("p t g -> p g t"),
-                        op0=ALU.mult,
-                        op1=ALU.add,
-                    )
-                    mean_of[s] = mean
                 nc.vector.scalar_tensor_tensor(
                     out=grouped[:, 1, j, :, :],
                     in0=grouped[:, 0, j, :, :],
@@ -253,40 +275,37 @@ def tile_gnnnicheencoder_pa_t_kernel(tc, h, W_l, b_l, W_r, ln_g, ln_b, out):
                 banks.append(acc)
             kept[("acc", q)] = banks
 
-        def add_bias(q):
-            c = work.tile([P, PAIR, D], F32, name="c", bufs=3)
-            row_sum = stats.tile([P, PAIR], F32, name="row_sum")
-            for j in range(PAIR):
-                nc.vector.scalar_tensor_tensor(
-                    out=c[:, j, :],
-                    in0=kept[("acc", q)][j][:],
-                    scalar=1.0,
-                    in1=bias_rows[:],
-                    op0=ALU.mult,
-                    op1=ALU.add,
-                    accum_out=row_sum[:, j : j + 1],
-                )
-            kept[("c", q)] = c
-            kept[("row_sum", q)] = row_sum
+        def add_bias(q, j):
+            if j == 0:
+                kept[("c", q)] = work.tile([P, PAIR, D], F32, name="c", bufs=3)
+                kept[("row_sum", q)] = stats.tile([P, PAIR], F32, name="row_sum")
+            nc.vector.scalar_tensor_tensor(
+                out=kept[("c", q)][:, j, :],
+                in0=kept[("acc", q)][j][:],
+                scalar=1.0,
+                in1=bias_rows[:],
+                op0=ALU.mult,
+                op1=ALU.add,
+                accum_out=kept[("row_sum", q)][:, j : j + 1],
+            )
 
         def negate_mean(q):
             minus_mean = stats.tile([P, PAIR], F32, name="minus_mean")
             nc.scalar.mul(out=minus_mean[:], in_=kept[("row_sum", q)][:], mul=-1.0 / D)
             kept[("minus_mean", q)] = minus_mean
 
-        def sum_squares(q):
-            square_sum = stats.tile([P, PAIR], F32, name="square_sum")
-            for j in range(PAIR):
-                squares = work.tile([P, D], BF16, name="squares")
-                nc.scalar.activation(
-                    out=squares[:],
-                    in_=kept[("c", q)][:, j, :],
-                    func=ACT.Square,
-                    bias=kept[("minus_mean", q)][:, j : j + 1],
-                    scale=1.0,
-                    accum_out=square_sum[:, j : j + 1],
-                )
-            kept[("square_sum", q)] = square_sum
+        def sum_squares(q, j):
+            if j == 0:
+                kept[("square_sum", q)] = stats.tile([P, PAIR], F32, name="square_sum")
+            squares = work.tile([P, D], BF16, name="squares")
+            nc.scalar.activation(
+                out=squares[:],
+                in_=kept[("c", q)][:, j, :],
+                func=ACT.Square,
+                bias=kept[("minus_mean", q)][:, j : j + 1],
+                scale=1.0,
+                accum_out=kept[("square_sum", q)][:, j : j + 1],
+            )
 
         def invert_deviation(q):
             inverse = stats.tile([P, PAIR], F32, name="inverse")
@@ -299,18 +318,24 @@ def tile_gnnnicheencoder_pa_t_kernel(tc, h, W_l, b_l, W_r, ln_g, ln_b, out):
             )
             kept[("inverse", q)] = inverse
 
-        def normalise(q):
-            normal = work.tile([P, PAIR, D], F32, name="normal")
-            for j in range(PAIR):
-                nc.gpsimd.tensor_scalar(
-                    out=normal[:, j, :],
-                    in0=kept[("c", q)][:, j, :],
-                    scalar1=kept[("minus_mean", q)][:, j : j + 1],
-                    scalar2=kept[("inverse", q)][:, j : j + 1],
-                    op0=ALU.add,
-                    op1=ALU.mult,
-                )
-            kept[("normal", q)] = normal
+        def admit(q):
+            minus_mean = stats.tile([P, PAIR], F32, name="minus_mean_again")
+            nc.vector.tensor_scalar_mul(
+                out=minus_mean[:], in0=kept[("row_sum", q)][:], scalar1=-1.0 / D
+            )
+            kept[("minus_mean_again", q)] = minus_mean
+
+        def normalise(q, j):
+            if j == 0:
+                kept[("normal", q)] = work.tile([P, PAIR, D], F32, name="normal")
+            nc.gpsimd.tensor_scalar(
+                out=kept[("normal", q)][:, j, :],
+                in0=kept[("c", q)][:, j, :],
+                scalar1=kept[("minus_mean_again", q)][:, j : j + 1],
+                scalar2=kept[("inverse", q)][:, j : j + 1],
+                op0=ALU.add,
+                op1=ALU.mult,
+            )
 
         def to_features(q):
             normal = kept[("normal", q)]
@@ -326,60 +351,55 @@ def tile_gnnnicheencoder_pa_t_kernel(tc, h, W_l, b_l, W_r, ln_g, ln_b, out):
                 banks.append(normal_turned)
             kept[("normal_turned", q)] = banks
 
-        def two_terms(q):
-            bent = work.tile([P, CHUNKS, PAIR, P], F32, name="bent")
-            straight = work.tile([P, CHUNKS, PAIR, P], F32, name="straight")
+        def two_terms(q, f):
+            if f == 0:
+                kept[("bent", q)] = work.tile([P, CHUNKS, PAIR, P], F32, name="bent")
+                kept[("straight", q)] = work.tile([P, CHUNKS, PAIR, P], F32, name="straight")
+            turned_chunk = kept[("normal_turned", q)][f // 2][:, f % 2, :, :]
+            nc.scalar.activation(
+                out=kept[("straight", q)][:, f, :, :],
+                in_=turned_chunk,
+                func=ACT.Identity,
+                bias=line_term[:, CHUNKS + f : CHUNKS + f + 1],
+                scale=line_term[:, f : f + 1],
+            )
+            nc.scalar.activation(
+                out=kept[("bent", q)][:, f, :, :],
+                in_=turned_chunk,
+                func=ACT.Relu,
+                bias=relu_term[:, CHUNKS + f : CHUNKS + f + 1],
+                scale=relu_term[:, f : f + 1],
+            )
+
+        def to_rows(q, j):
+            bent, straight = kept[("bent", q)], kept[("straight", q)]
+            a_rows = rows_pool.tile([P, D], F32)
             for f in range(CHUNKS):
-                normal_turned = kept[("normal_turned", q)][f // 2][:, f % 2, :, :]
-                nc.scalar.activation(
-                    out=bent[:, f, :, :],
-                    in_=normal_turned,
-                    func=ACT.Relu,
-                    bias=relu_term[:, CHUNKS + f : CHUNKS + f + 1],
-                    scale=relu_term[:, f : f + 1],
+                nc.tensor.matmul(
+                    out=a_rows[:, f * P : (f + 1) * P],
+                    lhsT=straight[:, f, j, :],
+                    rhs=identity[:],
+                    is_transpose=True,
+                    start=True,
+                    stop=False,
                 )
-                nc.scalar.activation(
-                    out=straight[:, f, :, :],
-                    in_=normal_turned,
-                    func=ACT.Identity,
-                    bias=line_term[:, CHUNKS + f : CHUNKS + f + 1],
-                    scale=line_term[:, f : f + 1],
+                nc.tensor.matmul(
+                    out=a_rows[:, f * P : (f + 1) * P],
+                    lhsT=bent[:, f, j, :],
+                    rhs=identity[:],
+                    is_transpose=True,
+                    start=False,
+                    stop=True,
                 )
-            kept[("terms", q)] = (bent, straight)
+            kept[("a_rows", q, j)] = a_rows
 
-        def to_rows(q):
-            bent, straight = kept[("terms", q)]
-            banks = []
-            for j in range(PAIR):
-                a_rows = rows_pool.tile([P, D], F32)
-                for f in range(CHUNKS):
-                    nc.tensor.matmul(
-                        out=a_rows[:, f * P : (f + 1) * P],
-                        lhsT=bent[:, f, j, :],
-                        rhs=identity[:],
-                        is_transpose=True,
-                        start=True,
-                        stop=False,
-                    )
-                    nc.tensor.matmul(
-                        out=a_rows[:, f * P : (f + 1) * P],
-                        lhsT=straight[:, f, j, :],
-                        rhs=identity[:],
-                        is_transpose=True,
-                        start=False,
-                        stop=True,
-                    )
-                banks.append(a_rows)
-            kept[("a_rows", q)] = banks
-
-        def add_residual(q):
-            for j in range(PAIR):
-                s, i = tiles[PAIR * q + j]
-                result = work.tile([P, D], F32, name="result", bufs=4)
-                nc.vector.tensor_add(
-                    out=result[:], in0=kept[("a_rows", q)][j][:], in1=by_graph[s][:, i, :]
-                )
-                nc.sync.dma_start(out=out[s * P : (s + 1) * P, i, :], in_=result[:])
+        def add_residual(q, j):
+            s, i = tiles[PAIR * q + j]
+            result = work.tile([P, D], F32, name="result", bufs=4)
+            nc.vector.tensor_add(
+                out=result[:], in0=kept[("a_rows", q, j)][:], in1=by_graph[s][:, i, :]
+            )
+            nc.sync.dma_start(out=out[s * P : (s + 1) * P, i, :], in_=result[:])
 
         def spread_vectors():
             vector_rows_f32 = const.tile([P, P], F32)
@@ -394,17 +414,19 @@ def tile_gnnnicheencoder_pa_t_kernel(tc, h, W_l, b_l, W_r, ln_g, ln_b, out):
             nc.vector.tensor_scalar_mul(out=line_term[:], in0=per_feature[:], scalar1=LEAKY_SLOPE)
             return relu_term, line_term
 
-        def run(stage_of_pair, q):
+        def run(stage_of_pair, q, *part):
             if 0 <= q < count:
-                stage_of_pair(q)
+                stage_of_pair(q, *part)
 
         row_sums = sums_pool.tile([P, D], F32, name="sums")
         turn(0)
         group(0)
-        add_nodes(row_sums, [LAST, *range(NODES_PER_LOAD)])
+        add_nodes(row_sums, range(*RUNS[0]))
+        add_nodes(row_sums, range(*RUNS[1]))
         turn(1)
         group(1)
-        add_nodes(row_sums, range(NODES_PER_LOAD, LAST))
+        for run_of_nodes in RUNS[2:]:
+            add_nodes(row_sums, range(*run_of_nodes))
         mean_rows = means.tile([P, D], F32, name="mean_rows", bufs=1)
         nc.scalar.copy(out=mean_rows[:], in_=row_sums[:])
         wr_grouped = turn_weight(nc, stage, features_pool, identity, wr_rows)
@@ -419,31 +441,38 @@ def tile_gnnnicheencoder_pa_t_kernel(tc, h, W_l, b_l, W_r, ln_g, ln_b, out):
         for k in range(HEAD, count + DEPTH):
             if k == 4:
                 relu_term, line_term = spread_vectors()
-            for s in range(1, BLOCKS):
-                since = k - max(pair_of_last[s - 1], HEAD)
-                if 0 <= since < GRAPHS_PER_SUM // LOADS_PER_STEP:
-                    for g in range(LOADS_PER_STEP * since, LOADS_PER_STEP * (since + 1)):
-                        load_nodes(s, g)
-                if since == GRAPHS_PER_SUM // LOADS_PER_STEP:
-                    load_graphs(s)
-            run(add_residual, k - 9)
-            run(add_bias, k - 4)
-            run(normalise, k - 6)
+            for s in range(2, BLOCKS):
+                since = k - first_pair[s - 1] + LOAD_AHEAD
+                if 0 <= since < len(RUNS):
+                    if s == 2:
+                        load_rows(s + 1, *RUNS[since])
+                    load_graphs(s, *RUNS[since])
+            run(add_residual, k - 9, 0)
+            run(add_residual, k - 9, 1)
+            run(add_bias, k - 4, 0)
+            run(add_bias, k - 4, 1)
+            run(normalise, k - 6, 0)
+            run(normalise, k - 6, 1)
             run(negate_mean, k - 5)
             if k > HEAD:
                 run(group, k - 1)
             run(to_features, k - 7)
-            run(to_rows, k - 8)
-            run(turn, k)
-            for s in range(1, BLOCKS):
-                first = pair_of_last[s] + 1 - SUMS // SUMS_PER_STEP
-                if first <= k < first + SUMS // SUMS_PER_STEP:
-                    for T in range(SUMS_PER_STEP * (k - first), SUMS_PER_STEP * (k - first + 1)):
-                        sum_nodes(s, T)
+            run(to_rows, k - 8, 0)
+            run(to_rows, k - 8, 1)
+            run(turn, k - 0)
+            sum_nodes(k)
             run(multiply, k - 3)
-            run(sum_squares, k - 5)
-            run(two_terms, k - 7)
+            run(sum_squares, k - 5, 0)
+            run(sum_squares, k - 5, 1)
+            run(two_terms, k - 7, 0)
+            run(two_terms, k - 7, 1)
+            run(two_terms, k - 7, 2)
+            run(two_terms, k - 7, 3)
             run(invert_deviation, k - 5)
             if k > HEAD:
                 run(quantise, k - 2)
+            if k > HEAD:
                 run(neighbours, k - 1)
+            while done_sums:
+                keep_mean(done_sums.pop(0))
+            run(admit, k - 5)

@@ -26,6 +26,7 @@ TOUCHED = 9
 LN_EPS = 1e-5
 LEAKY_SLOPE = 0.01
 PAIR = 2
+ALONE = 4
 RUNS = [(0, 1), (1, 5), (5, 9), (9, 13), (13, 17)]
 LOAD_AHEAD = 1
 EARLY_PASSES = 12
@@ -43,7 +44,7 @@ def turn_words(nc, identity, rows, turned):
 
 
 def group_words(nc, turned, grouped):
-    nc.scalar.copy(out=grouped.bitcast(F32), in_=turned[:].rearrange("p j u r -> p j r u"))
+    nc.scalar.copy(out=grouped.bitcast(F32), in_=turned.rearrange("p j u r -> p j r u"))
 
 
 def load_weight(nc, stage, weight):
@@ -59,7 +60,7 @@ def turn_weight(nc, stage, turned_pool, identity, rows):
         for j in range(PAIR):
             turn_words(nc, identity, rows[:, a + j, :], turned[:, j, :, :])
         group_words(
-            nc, turned, grouped[:, a * P : (a + PAIR) * P, :].rearrange("p (j o) t -> p j o t", j=PAIR)
+            nc, turned[:], grouped[:, a * P : (a + PAIR) * P, :].rearrange("p (j o) t -> p j o t", j=PAIR)
         )
     return grouped
 
@@ -155,8 +156,10 @@ def tile_gnnnicheencoder_pa_t_kernel(tc, h, W_l, b_l, W_r, ln_g, ln_b, out):
             load_graphs(1, *run_of_nodes)
 
         tiles = [(s, i) for s in range(BLOCKS) for i in range(NODES)]
-        count = len(tiles) // PAIR
-        first_pair = [s * NODES // PAIR for s in range(BLOCKS)]
+        teams = [[tile] for tile in tiles[:ALONE]]
+        teams += [tiles[x : x + PAIR] for x in range(ALONE, len(tiles), PAIR)]
+        count = len(teams)
+        first_team = [[(s, 0) in team for team in teams].index(True) for s in range(BLOCKS)]
         sums_of = {}
         mean_of = {}
         kept = {}
@@ -165,7 +168,8 @@ def tile_gnnnicheencoder_pa_t_kernel(tc, h, W_l, b_l, W_r, ln_g, ln_b, out):
         done_sums = []
 
         def sum_nodes(k):
-            for x in range(EARLY_PASSES if k < DEPTH else LATE_PASSES):
+            size = len(teams[k]) if k < count else PAIR
+            for x in range((EARLY_PASSES if k < first_team[1] else LATE_PASSES) * size // 2):
                 if sum_passes:
                     s, t, T = sum_passes.pop(0)
                     sum_node(s, t, T)
@@ -216,20 +220,19 @@ def tile_gnnnicheencoder_pa_t_kernel(tc, h, W_l, b_l, W_r, ln_g, ln_b, out):
 
         def turn(q):
             turned = turned_pool.tile([P, PAIR, HALVES, P], F32)
-            for j in range(PAIR):
-                s, i = tiles[PAIR * q + j]
+            for j, (s, i) in enumerate(teams[q]):
                 turn_words(nc, identity, by_graph[s][:, i, :], turned[:, j, :, :])
             kept[("turned", q)] = turned
 
         def group(q):
-            grouped = work.tile([P, 2, PAIR, P, PACK], BF16, name="grouped", align_bytes=64, bufs=3)
-            group_words(nc, kept[("turned", q)], grouped[:, 0, :, :, :])
+            size = len(teams[q])
+            grouped = work.tile([P, 2, size, P, PACK], BF16, name="grouped", align_bytes=64, bufs=3)
+            group_words(nc, kept[("turned", q)][:, 0:size, :, :], grouped[:, 0, :, :, :])
             kept[("grouped", q)] = grouped
 
         def neighbours(q):
             grouped = kept[("grouped", q)]
-            for j in range(PAIR):
-                s, i = tiles[PAIR * q + j]
+            for j, (s, i) in enumerate(teams[q]):
                 nc.vector.scalar_tensor_tensor(
                     out=grouped[:, 1, j, :, :],
                     in0=grouped[:, 0, j, :, :],
@@ -240,8 +243,8 @@ def tile_gnnnicheencoder_pa_t_kernel(tc, h, W_l, b_l, W_r, ln_g, ln_b, out):
                 )
 
         def quantise(q):
-            codes = work.tile([P, 2, PAIR, P], U32, name="codes", align_bytes=64)
-            scales = work.tile([P, 2, PAIR, P], U8, name="scales", align_bytes=64)
+            codes = work.tile([P, 2, len(teams[q]), P], U32, name="codes", align_bytes=64)
+            scales = work.tile([P, 2, len(teams[q]), P], U8, name="scales", align_bytes=64)
             nc.vector.quantize_mx(
                 out=codes[:].rearrange("p x j r -> p (x j r)").bitcast(FP8X4),
                 scales=scales[:].rearrange("p x j r -> p (x j r)"),
@@ -252,7 +255,7 @@ def tile_gnnnicheencoder_pa_t_kernel(tc, h, W_l, b_l, W_r, ln_g, ln_b, out):
         def multiply(q):
             codes, scales = kept[("codes", q)]
             banks = []
-            for j in range(PAIR):
+            for j in range(len(teams[q])):
                 acc = acc_pool.tile([P, D], F32)
                 nc.tensor.matmul_mx(
                     out=acc[:],
@@ -289,11 +292,6 @@ def tile_gnnnicheencoder_pa_t_kernel(tc, h, W_l, b_l, W_r, ln_g, ln_b, out):
                 accum_out=kept[("row_sum", q)][:, j : j + 1],
             )
 
-        def negate_mean(q):
-            minus_mean = stats.tile([P, PAIR], F32, name="minus_mean")
-            nc.scalar.mul(out=minus_mean[:], in_=kept[("row_sum", q)][:], mul=-1.0 / D)
-            kept[("minus_mean", q)] = minus_mean
-
         def sum_squares(q, j):
             if j == 0:
                 kept[("square_sum", q)] = stats.tile([P, PAIR], F32, name="square_sum")
@@ -302,26 +300,27 @@ def tile_gnnnicheencoder_pa_t_kernel(tc, h, W_l, b_l, W_r, ln_g, ln_b, out):
                 out=squares[:],
                 in_=kept[("c", q)][:, j, :],
                 func=ACT.Square,
-                bias=kept[("minus_mean", q)][:, j : j + 1],
-                scale=1.0,
+                bias=kept[("row_sum", q)][:, j : j + 1],
+                scale=-float(D),
                 accum_out=kept[("square_sum", q)][:, j : j + 1],
             )
 
         def invert_deviation(q):
             inverse = stats.tile([P, PAIR], F32, name="inverse")
             nc.scalar.activation(
-                out=inverse[:],
-                in_=kept[("square_sum", q)][:],
+                out=inverse[:, 0 : len(teams[q])],
+                in_=kept[("square_sum", q)][:, 0 : len(teams[q])],
                 func=ACT.Abs_reciprocal_sqrt,
                 bias=eps[:],
-                scale=1.0 / D,
+                scale=1.0 / D**3,
             )
             kept[("inverse", q)] = inverse
 
         def admit(q):
             minus_mean = stats.tile([P, PAIR], F32, name="minus_mean_again")
+            size = len(teams[q])
             nc.vector.tensor_scalar_mul(
-                out=minus_mean[:], in0=kept[("row_sum", q)][:], scalar1=-1.0 / D
+                out=minus_mean[:, 0:size], in0=kept[("row_sum", q)][:, 0:size], scalar1=-1.0 / D
             )
             kept[("minus_mean_again", q)] = minus_mean
 
@@ -344,7 +343,7 @@ def tile_gnnnicheencoder_pa_t_kernel(tc, h, W_l, b_l, W_r, ln_g, ln_b, out):
                 normal_turned = features_pool.tile([P, 2, PAIR, P], F32)
                 for x in range(2):
                     f = 2 * half + x
-                    for j in range(PAIR):
+                    for j in range(len(teams[q])):
                         nc.tensor.transpose(
                             normal_turned[:, x, j, :], normal[:, j, f * P : (f + 1) * P], identity[:]
                         )
@@ -355,16 +354,17 @@ def tile_gnnnicheencoder_pa_t_kernel(tc, h, W_l, b_l, W_r, ln_g, ln_b, out):
             if f == 0:
                 kept[("bent", q)] = work.tile([P, CHUNKS, PAIR, P], F32, name="bent")
                 kept[("straight", q)] = work.tile([P, CHUNKS, PAIR, P], F32, name="straight")
-            turned_chunk = kept[("normal_turned", q)][f // 2][:, f % 2, :, :]
+            size = len(teams[q])
+            turned_chunk = kept[("normal_turned", q)][f // 2][:, f % 2, 0:size, :]
             nc.scalar.activation(
-                out=kept[("straight", q)][:, f, :, :],
+                out=kept[("straight", q)][:, f, 0:size, :],
                 in_=turned_chunk,
                 func=ACT.Identity,
                 bias=line_term[:, CHUNKS + f : CHUNKS + f + 1],
                 scale=line_term[:, f : f + 1],
             )
             nc.scalar.activation(
-                out=kept[("bent", q)][:, f, :, :],
+                out=kept[("bent", q)][:, f, 0:size, :],
                 in_=turned_chunk,
                 func=ACT.Relu,
                 bias=relu_term[:, CHUNKS + f : CHUNKS + f + 1],
@@ -394,7 +394,7 @@ def tile_gnnnicheencoder_pa_t_kernel(tc, h, W_l, b_l, W_r, ln_g, ln_b, out):
             kept[("a_rows", q, j)] = a_rows
 
         def add_residual(q, j):
-            s, i = tiles[PAIR * q + j]
+            s, i = teams[q][j]
             result = work.tile([P, D], F32, name="result", bufs=4)
             nc.vector.tensor_add(
                 out=result[:], in0=kept[("a_rows", q, j)][:], in1=by_graph[s][:, i, :]
@@ -414,9 +414,19 @@ def tile_gnnnicheencoder_pa_t_kernel(tc, h, W_l, b_l, W_r, ln_g, ln_b, out):
             nc.vector.tensor_scalar_mul(out=line_term[:], in0=per_feature[:], scalar1=LEAKY_SLOPE)
             return relu_term, line_term
 
-        def run(stage_of_pair, q, *part):
+        def run(stage, q):
             if 0 <= q < count:
-                stage_of_pair(q, *part)
+                stage(q)
+
+        def run_tiles(stage, q):
+            if 0 <= q < count:
+                for j in range(len(teams[q])):
+                    stage(q, j)
+
+        def run_parts(stage, q):
+            if 0 <= q < count:
+                for f in range(CHUNKS):
+                    stage(q, f)
 
         row_sums = sums_pool.tile([P, D], F32, name="sums")
         turn(0)
@@ -442,32 +452,23 @@ def tile_gnnnicheencoder_pa_t_kernel(tc, h, W_l, b_l, W_r, ln_g, ln_b, out):
             if k == 4:
                 relu_term, line_term = spread_vectors()
             for s in range(2, BLOCKS):
-                since = k - first_pair[s - 1] + LOAD_AHEAD
+                since = k - first_team[s - 1] + LOAD_AHEAD
                 if 0 <= since < len(RUNS):
                     if s == 2:
                         load_rows(s + 1, *RUNS[since])
                     load_graphs(s, *RUNS[since])
-            run(add_residual, k - 9, 0)
-            run(add_residual, k - 9, 1)
-            run(add_bias, k - 4, 0)
-            run(add_bias, k - 4, 1)
-            run(normalise, k - 6, 0)
-            run(normalise, k - 6, 1)
-            run(negate_mean, k - 5)
+            run_tiles(add_residual, k - 9)
+            run_tiles(add_bias, k - 4)
+            run_tiles(normalise, k - 6)
             if k > HEAD:
                 run(group, k - 1)
             run(to_features, k - 7)
-            run(to_rows, k - 8, 0)
-            run(to_rows, k - 8, 1)
-            run(turn, k - 0)
+            run_tiles(to_rows, k - 8)
+            run(turn, k)
             sum_nodes(k)
             run(multiply, k - 3)
-            run(sum_squares, k - 5, 0)
-            run(sum_squares, k - 5, 1)
-            run(two_terms, k - 7, 0)
-            run(two_terms, k - 7, 1)
-            run(two_terms, k - 7, 2)
-            run(two_terms, k - 7, 3)
+            run_tiles(sum_squares, k - 5)
+            run_parts(two_terms, k - 7)
             run(invert_deviation, k - 5)
             if k > HEAD:
                 run(quantise, k - 2)

@@ -27,10 +27,12 @@ LN_EPS = 1e-5
 LEAKY_SLOPE = 0.01
 PAIR = 2
 ALONE = 4
-RUNS = [(0, 1), (1, 5), (5, 9), (9, 13), (13, 17)]
+RUNS = [(0, 1), (1, 5), (5, 9), (9, 13), (13, 15), (15, 17)]
 LOAD_AHEAD = 1
 EARLY_PASSES = 12
 LATE_PASSES = 9
+WARM_UP = 5
+AHEAD = 2
 HEAD = 2
 DEPTH = 9
 
@@ -91,6 +93,10 @@ def tile_gnnnicheencoder_pa_t_kernel(tc, h, W_l, b_l, W_r, ln_g, ln_b, out):
 
         identity = const.tile([P, P], F32)
         make_identity(nc, identity[:])
+        nothing = const.tile([P, D], BF16)
+        nc.vector.memset(nothing[:].bitcast(I32), 0)
+        sixteenth = const.tile([P, P], BF16)
+        nc.vector.tensor_scalar_mul(out=sixteenth[:], in0=identity[:], scalar1=1.0 / OTHERS)
         diagonal = const.tile([P, NODES + TOUCHED * NODES], F32)
         nc.vector.memset(diagonal[:], 0.0)
         nc.vector.tensor_copy(out=diagonal[:, NODES : NODES + P], in_=identity[:])
@@ -107,10 +113,6 @@ def tile_gnnnicheencoder_pa_t_kernel(tc, h, W_l, b_l, W_r, ln_g, ln_b, out):
             )
         graph_sum = const.tile([P, NODES, TOUCHED], BF16)
         nc.vector.tensor_scalar_mul(out=graph_sum[:], in0=graph_of_row[:], scalar1=1.0 / OTHERS)
-        nothing = const.tile([P, P], BF16)
-        nc.vector.memset(nothing[:].bitcast(I32), 0)
-        sixteenth = const.tile([P, P], BF16)
-        nc.vector.tensor_scalar_mul(out=sixteenth[:], in0=identity[:], scalar1=1.0 / OTHERS)
         eps = const.tile([P, 1], F32)
         nc.vector.memset(eps[:], LN_EPS)
         vector_rows = const.tile([P, P], BF16)
@@ -164,36 +166,43 @@ def tile_gnnnicheencoder_pa_t_kernel(tc, h, W_l, b_l, W_r, ln_g, ln_b, out):
         mean_of = {}
         kept = {}
 
-        sum_passes = [(s, t, T) for s in range(1, BLOCKS) for t in range(PACK) for T in range(NODES)]
-        done_sums = []
-
-        def sum_nodes(k):
-            size = len(teams[k]) if k < count else PAIR
-            for x in range((EARLY_PASSES if k < first_team[1] else LATE_PASSES) * size // 2):
-                if sum_passes:
-                    s, t, T = sum_passes.pop(0)
-                    sum_node(s, t, T)
-                    if (t, T) == (PACK - 1, NODES - 1):
-                        done_sums.append(s)
-                        if sum_passes:
-                            return
-
-        def sum_node(s, t, T):
-            if t == 0 and T == 0:
-                sums_of[s] = sums_pool.tile([P, PACK, P], F32, name="sums")
-            if T == 0:
-                nc.tensor.matmul(
-                    out=sums_of[s][:, t, :], lhsT=sixteenth[:], rhs=nothing[:], start=True, stop=False
-                )
-            begin = T * P // NODES
-            end = min(begin + TOUCHED, P)
+        def sum_nodes(s, c):
+            if c == 0:
+                sums_of[s] = sums_pool.tile([P, CHUNKS, P], F32, name="sums")
             nc.tensor.matmul(
-                out=sums_of[s][:, t, begin:end],
-                lhsT=by_row[s][:, T, :].rearrange("p (q t) -> p t q", t=PACK)[:, t, :],
-                rhs=graph_sum[:, T, 0 : end - begin],
-                start=False,
-                stop=(T == NODES - 1),
+                out=sums_of[s][:, c, :], lhsT=sixteenth[:], rhs=nothing[:, 0:P], start=True, stop=False
             )
+            for T in range(NODES):
+                begin = T * P // NODES
+                end = min(begin + TOUCHED, P)
+                nc.tensor.matmul(
+                    out=sums_of[s][:, c, begin:end],
+                    lhsT=by_row[s][:, T, c * P : (c + 1) * P],
+                    rhs=graph_sum[:, T, 0 : end - begin],
+                    start=False,
+                    stop=(T == NODES - 1),
+                )
+
+        def keep_sums(s):
+            sums = means.tile([P, CHUNKS, P], F32, name="sums_kept", bufs=1)
+            nc.vector.tensor_copy(out=sums[:], in_=sums_of[s][:])
+            kept[("sums", s)] = sums
+
+        def sums_to_rows(s):
+            rows = sums_pool.tile([P, D], F32, name="sums")
+            for c in range(CHUNKS):
+                nc.tensor.transpose(rows[:, c * P : (c + 1) * P], kept[("sums", s)][:, c, :], identity[:])
+            kept[("sum_rows", s)] = rows
+
+        def keep_rows(s):
+            rows = means.tile([P, D], F32, name="mean_rows", bufs=1)
+            nc.scalar.copy(out=rows[:], in_=kept[("sum_rows", s)][:])
+            kept[("mean_rows", s)] = rows
+
+        def turn_rows(s):
+            sums_of[s] = sums_pool.tile([P, PACK, P], F32, name="sums")
+            for t in range(PACK):
+                nc.tensor.transpose(sums_of[s][:, t, :], kept[("mean_rows", s)][:, t::PACK], identity[:])
 
         def keep_mean(s):
             mean = means.tile([P, P, PACK], F32, name="mean")
@@ -226,7 +235,7 @@ def tile_gnnnicheencoder_pa_t_kernel(tc, h, W_l, b_l, W_r, ln_g, ln_b, out):
 
         def group(q):
             size = len(teams[q])
-            grouped = work.tile([P, 2, size, P, PACK], BF16, name="grouped", align_bytes=64, bufs=3)
+            grouped = work.tile([P, 2, size, P, PACK], BF16, name="grouped", align_bytes=64, bufs=3 + AHEAD)
             group_words(nc, kept[("turned", q)][:, 0:size, :, :], grouped[:, 0, :, :, :])
             kept[("grouped", q)] = grouped
 
@@ -429,14 +438,22 @@ def tile_gnnnicheencoder_pa_t_kernel(tc, h, W_l, b_l, W_r, ln_g, ln_b, out):
                     stage(q, f)
 
         row_sums = sums_pool.tile([P, D], F32, name="sums")
+        for x in range(WARM_UP):
+            nc.tensor.matmul(out=row_sums[:], lhsT=sixteenth[:], rhs=nothing[:], start=True, stop=True)
         turn(0)
         group(0)
         add_nodes(row_sums, range(*RUNS[0]))
         add_nodes(row_sums, range(*RUNS[1]))
         turn(1)
         group(1)
-        for run_of_nodes in RUNS[2:]:
+        for x, run_of_nodes in enumerate(RUNS[2:]):
             add_nodes(row_sums, range(*run_of_nodes))
+            if x < AHEAD:
+                turn(2 + x)
+                group(2 + x)
+        for x in range(len(RUNS[2:]), AHEAD):
+            turn(2 + x)
+            group(2 + x)
         mean_rows = means.tile([P, D], F32, name="mean_rows", bufs=1)
         nc.scalar.copy(out=mean_rows[:], in_=row_sums[:])
         wr_grouped = turn_weight(nc, stage, features_pool, identity, wr_rows)
@@ -461,11 +478,21 @@ def tile_gnnnicheencoder_pa_t_kernel(tc, h, W_l, b_l, W_r, ln_g, ln_b, out):
             run_tiles(add_bias, k - 4)
             run_tiles(normalise, k - 6)
             if k > HEAD:
-                run(group, k - 1)
+                run(group, k - 1 + AHEAD)
+            for s in range(1, BLOCKS):
+                if k == first_team[s]:
+                    keep_rows(s)
             run(to_features, k - 7)
             run_tiles(to_rows, k - 8)
-            run(turn, k)
-            sum_nodes(k)
+            run(turn, k + AHEAD)
+            for s in range(1, BLOCKS):
+                since = k - first_team[s] + 1 + CHUNKS
+                if 0 <= since < CHUNKS:
+                    sum_nodes(s, since)
+                if since == CHUNKS:
+                    sums_to_rows(s)
+                if since == CHUNKS + 1:
+                    turn_rows(s)
             run(multiply, k - 3)
             run_tiles(sum_squares, k - 5)
             run_parts(two_terms, k - 7)
@@ -474,6 +501,9 @@ def tile_gnnnicheencoder_pa_t_kernel(tc, h, W_l, b_l, W_r, ln_g, ln_b, out):
                 run(quantise, k - 2)
             if k > HEAD:
                 run(neighbours, k - 1)
-            while done_sums:
-                keep_mean(done_sums.pop(0))
+            for s in range(1, BLOCKS):
+                if k == first_team[s] - 2:
+                    keep_sums(s)
+                if k == first_team[s]:
+                    keep_mean(s)
             run(admit, k - 5)

@@ -185,7 +185,7 @@ def tile_gnnnicheencoder_pa_t_kernel(tc, h, W_l, b_l, W_r, ln_g, ln_b, out):
 
         def keep_sums(s):
             sums = means.tile([P, CHUNKS, P], F32, name="sums_kept", bufs=1)
-            nc.vector.tensor_copy(out=sums[:], in_=sums_of[s][:])
+            nc.scalar.copy(out=sums[:], in_=sums_of[s][:])
             kept[("sums", s)] = sums
 
         def sums_to_rows(s):
@@ -206,7 +206,7 @@ def tile_gnnnicheencoder_pa_t_kernel(tc, h, W_l, b_l, W_r, ln_g, ln_b, out):
 
         def keep_mean(s):
             mean = means.tile([P, P, PACK], F32, name="mean")
-            nc.vector.tensor_copy(out=mean[:], in_=sums_of[s][:].rearrange("p t g -> p g t"))
+            nc.scalar.copy(out=mean[:], in_=sums_of[s][:].rearrange("p t g -> p g t"))
             mean_of[s] = mean
 
         def add_nodes(row_sums, nodes):
@@ -240,13 +240,17 @@ def tile_gnnnicheencoder_pa_t_kernel(tc, h, W_l, b_l, W_r, ln_g, ln_b, out):
             kept[("grouped", q)] = grouped
 
         def neighbours(q):
-            grouped = kept[("grouped", q)]
-            for j, (s, i) in enumerate(teams[q]):
+            grouped = kept[("grouped", q)][:].rearrange("p x j r t -> p x j (r t)")
+            for s in range(BLOCKS):
+                mine = [j for j, tile in enumerate(teams[q]) if tile[0] == s]
+                if not mine:
+                    continue
+                mean = mean_of[s][:].rearrange("p g t -> p (g t)").unsqueeze(1)
                 nc.vector.scalar_tensor_tensor(
-                    out=grouped[:, 1, j, :, :],
-                    in0=grouped[:, 0, j, :, :],
+                    out=grouped[:, 1, mine[0] : mine[-1] + 1, :],
+                    in0=grouped[:, 0, mine[0] : mine[-1] + 1, :],
                     scalar=-1.0 / OTHERS,
-                    in1=mean_of[s][:],
+                    in1=mean.to_broadcast([P, len(mine), D]),
                     op0=ALU.mult,
                     op1=ALU.add,
                 )
@@ -432,9 +436,9 @@ def tile_gnnnicheencoder_pa_t_kernel(tc, h, W_l, b_l, W_r, ln_g, ln_b, out):
                 for j in range(len(teams[q])):
                     stage(q, j)
 
-        def run_parts(stage, q):
+        def run_parts(stage, q, begin, end):
             if 0 <= q < count:
-                for f in range(CHUNKS):
+                for f in range(begin, end):
                     stage(q, f)
 
         row_sums = sums_pool.tile([P, D], F32, name="sums")
@@ -480,6 +484,8 @@ def tile_gnnnicheencoder_pa_t_kernel(tc, h, W_l, b_l, W_r, ln_g, ln_b, out):
             if k > HEAD:
                 run(group, k - 1 + AHEAD)
             for s in range(1, BLOCKS):
+                if k == first_team[s] - 1:
+                    keep_sums(s)
                 if k == first_team[s]:
                     keep_rows(s)
             run(to_features, k - 7)
@@ -495,15 +501,14 @@ def tile_gnnnicheencoder_pa_t_kernel(tc, h, W_l, b_l, W_r, ln_g, ln_b, out):
                     turn_rows(s)
             run(multiply, k - 3)
             run_tiles(sum_squares, k - 5)
-            run_parts(two_terms, k - 7)
+            run_parts(two_terms, k - 7, 0, 1)
             run(invert_deviation, k - 5)
+            run_parts(two_terms, k - 7, 1, CHUNKS)
+            for s in range(1, BLOCKS):
+                if k == first_team[s]:
+                    keep_mean(s)
             if k > HEAD:
                 run(quantise, k - 2)
             if k > HEAD:
                 run(neighbours, k - 1)
-            for s in range(1, BLOCKS):
-                if k == first_team[s] - 2:
-                    keep_sums(s)
-                if k == first_team[s]:
-                    keep_mean(s)
             run(admit, k - 5)

from contextlib import ExitStack

import concourse.mybir as mybir
from concourse.masks import make_identity

F32 = mybir.dt.float32
BF16 = mybir.dt.bfloat16
I32 = mybir.dt.int32
U32 = mybir.dt.uint32
U8 = mybir.dt.uint8
FP8X4 = mybir.dt.float8_e4m3fn_x4
ALU = mybir.AluOpType
ACT = mybir.ActivationFunctionType
AXIS = mybir.AxisListType

P = 128
PACK = 4
HALVES = 2
GRAPHS = 512
NODES = 17
D = 512
CHUNKS = D // P
BLOCKS = GRAPHS // P
OTHERS = NODES - 1
TOUCHED = 9
LN_EPS = 1e-5
LEAKY_SLOPE = 0.01
PAIR = 2
ALONE = 4
RUNS = [(0, 1), (1, 5), (5, 9), (9, 13), (13, 15), (15, 17)]
LOAD_AHEAD = 1
EARLY_PASSES = 12
LATE_PASSES = 9
WARM_UP = 5
AHEAD = 2
HEAD = 2
DEPTH = 9

FLOPS = 2 * 2 * GRAPHS * NODES * D * D


def turn_words(nc, identity, rows, turned):
    words = rows.bitcast(F32)
    for u in range(HALVES):
        nc.tensor.transpose(turned[:, u, :], words[:, u::HALVES], identity[:])


def group_words(nc, turned, grouped):
    nc.scalar.copy(out=grouped.bitcast(F32), in_=turned.rearrange("p j u r -> p j r u"))


def load_weight(nc, stage, weight):
    rows = stage.tile([P, CHUNKS, D], BF16, name="weight_rows")
    nc.sync.dma_start(out=rows[:], in_=weight.rearrange("(a p) k -> p a k", p=P))
    return rows


def turn_weight(nc, stage, turned_pool, identity, rows):
    grouped = stage.tile([P, D, PACK], BF16, name="weight_grouped", align_bytes=64)
    for a in range(0, CHUNKS, PAIR):
        turned = turned_pool.tile([P, PAIR, HALVES, P], F32, name="normal_turned")
        for j in range(PAIR):
            turn_words(nc, identity, rows[:, a + j, :], turned[:, j, :, :])
        group_words(
            nc, turned[:], grouped[:, a * P : (a + PAIR) * P, :].rearrange("p (j o) t -> p j o t", j=PAIR)
        )
    return grouped


def quantise_weight(nc, grouped, codes, scales):
    nc.vector.quantize_mx(
        out=codes[:].bitcast(FP8X4),
        scales=scales[:],
        in_=grouped[:].rearrange("p o t -> p (o t)"),
    )


def tile_gnnnicheencoder_pa_t_kernel(tc, h, W_l, b_l, W_r, ln_g, ln_b, out):
    nc = tc.nc
    with ExitStack() as stack:
        stack.enter_context(tc.manual_schedule())
        const = stack.enter_context(tc.tile_pool(name="const", bufs=1))
        stage = stack.enter_context(tc.tile_pool(name="stage", bufs=2))
        blocks = stack.enter_context(tc.tile_pool(name="blocks", bufs=BLOCKS))
        means = stack.enter_context(tc.tile_pool(name="means", bufs=BLOCKS))
        work = stack.enter_context(tc.tile_pool(name="work", bufs=2))
        stats = stack.enter_context(tc.tile_pool(name="stats", bufs=4))
        turned_pool = stack.enter_context(tc.psum_pool(name="turned", bufs=1))
        sums_pool = stack.enter_context(tc.psum_pool(name="sums", bufs=1))
        acc_pool = stack.enter_context(tc.psum_pool(name="acc", bufs=PAIR))
        features_pool = stack.enter_context(tc.psum_pool(name="features", bufs=PAIR))
        rows_pool = stack.enter_context(tc.psum_pool(name="rows", bufs=PAIR))

        identity = const.tile([P, P], F32)
        make_identity(nc, identity[:])
        nothing = const.tile([P, D], BF16)
        nc.vector.memset(nothing[:].bitcast(I32), 0)
        sixteenth = const.tile([P, P], BF16)
        nc.vector.tensor_scalar_mul(out=sixteenth[:], in0=identity[:], scalar1=1.0 / OTHERS)
        diagonal = const.tile([P, NODES + TOUCHED * NODES], F32)
        nc.vector.memset(diagonal[:], 0.0)
        nc.vector.tensor_copy(out=diagonal[:, NODES : NODES + P], in_=identity[:])
        graph_of_row = const.tile([P, NODES, TOUCHED], F32)
        for T in range(NODES):
            before = T * P % NODES
            nc.vector.tensor_reduce(
                out=graph_of_row[:, T, :],
                in_=diagonal[:, NODES - before : NODES - before + TOUCHED * NODES].rearrange(
                    "p (j i) -> p j i", i=NODES
                ),
                axis=AXIS.X,
                op=ALU.add,
            )
        graph_sum = const.tile([P, NODES, TOUCHED], BF16)
        nc.vector.tensor_scalar_mul(out=graph_sum[:], in0=graph_of_row[:], scalar1=1.0 / OTHERS)
        eps = const.tile([P, 1], F32)
        nc.vector.memset(eps[:], LN_EPS)
        vector_rows = const.tile([P, P], BF16)
        nc.vector.memset(vector_rows[:].bitcast(I32), 0)

        wr_codes = const.tile([P, D], U32, align_bytes=64)
        wr_scales = const.tile([P, D], U8, align_bytes=64)
        wl_codes = const.tile([P, D], U32, align_bytes=64)
        wl_scales = const.tile([P, D], U8, align_bytes=64)

        by_graph = {}
        by_row = {}

        def load_graphs(s, begin, end):
            if begin == 0:
                by_graph[s] = blocks.tile([P, NODES, D], BF16, name="by_graph")
            nc.sync.dma_start(
                out=by_graph[s][:, begin:end, :], in_=h[s * P : (s + 1) * P, begin:end, :]
            )

        def load_rows(s, begin, end):
            if begin == 0:
                by_row[s] = blocks.tile([P, NODES, D], BF16, name="by_row", bufs=BLOCKS - 1)
            lines = h[s * P : (s + 1) * P, :, :].rearrange("g i k -> (g i) k")
            lines = lines.rearrange("(T p) k -> p T k", p=P)
            nc.sync.dma_start(out=by_row[s][:, begin:end, :], in_=lines[:, begin:end, :])

        for run_of_nodes in RUNS:
            load_graphs(0, *run_of_nodes)
        wr_rows = load_weight(nc, stage, W_r)
        wl_rows = load_weight(nc, stage, W_l)
        bias_rows = const.tile([P, D], BF16)
        nc.sync.dma_start(out=bias_rows[:], in_=b_l.partition_broadcast(P))
        nc.sync.dma_start(out=vector_rows[0:CHUNKS, :], in_=ln_g.rearrange("(f p) -> f p", p=P))
        nc.sync.dma_start(
            out=vector_rows[CHUNKS : 2 * CHUNKS, :], in_=ln_b.rearrange("(f p) -> f p", p=P)
        )
        for run_of_nodes in RUNS:
            load_rows(1, *run_of_nodes)
        for run_of_nodes in RUNS:
            load_rows(2, *run_of_nodes)
        for run_of_nodes in RUNS:
            load_graphs(1, *run_of_nodes)

        tiles = [(s, i) for s in range(BLOCKS) for i in range(NODES)]
        teams = [[tile] for tile in tiles[:ALONE]]
        teams += [tiles[x : x + PAIR] for x in range(ALONE, len(tiles), PAIR)]
        count = len(teams)
        first_team = [[(s, 0) in team for team in teams].index(True) for s in range(BLOCKS)]
        sums_of = {}
        mean_of = {}
        kept = {}

        def sum_nodes(s, c):
            if c == 0:
                sums_of[s] = sums_pool.tile([P, CHUNKS, P], F32, name="sums")
            nc.tensor.matmul(
                out=sums_of[s][:, c, :], lhsT=sixteenth[:], rhs=nothing[:, 0:P], start=True, stop=False
            )
            for T in range(NODES):
                begin = T * P // NODES
                end = min(begin + TOUCHED, P)
                nc.tensor.matmul(
                    out=sums_of[s][:, c, begin:end],
                    lhsT=by_row[s][:, T, c * P : (c + 1) * P],
                    rhs=graph_sum[:, T, 0 : end - begin],
                    start=False,
                    stop=(T == NODES - 1),
                )

        def keep_sums(s):
            sums = means.tile([P, CHUNKS, P], F32, name="sums_kept", bufs=1)
            nc.scalar.copy(out=sums[:], in_=sums_of[s][:])
            kept[("sums", s)] = sums

        def sums_to_rows(s):
            rows = sums_pool.tile([P, D], F32, name="sums")
            for c in range(CHUNKS):
                nc.tensor.transpose(rows[:, c * P : (c + 1) * P], kept[("sums", s)][:, c, :], identity[:])
            kept[("sum_rows", s)] = rows

        def keep_rows(s):
            rows = means.tile([P, D], F32, name="mean_rows", bufs=1)
            nc.scalar.copy(out=rows[:], in_=kept[("sum_rows", s)][:])
            kept[("mean_rows", s)] = rows

        def turn_rows(s):
            sums_of[s] = sums_pool.tile([P, PACK, P], F32, name="sums")
            for t in range(PACK):
                nc.tensor.transpose(sums_of[s][:, t, :], kept[("mean_rows", s)][:, t::PACK], identity[:])

        def keep_mean(s):
            mean = means.tile([P, P, PACK], F32, name="mean")
            nc.scalar.copy(out=mean[:], in_=sums_of[s][:].rearrange("p t g -> p g t"))
            mean_of[s] = mean

        def add_nodes(row_sums, nodes):
            for i in nodes:
                nc.tensor.matmul(
                    out=row_sums[:],
                    lhsT=sixteenth[:],
                    rhs=by_graph[0][:, i, :],
                    start=(i == 0),
                    stop=(i == NODES - 1),
                )

        def turn_mean(mean_rows):
            mean_turned = sums_pool.tile([P, PACK, P], F32, name="sums")
            for t in range(PACK):
                nc.tensor.transpose(mean_turned[:, t, :], mean_rows[:, t::PACK], identity[:])
            mean = means.tile([P, P, PACK], F32, name="mean")
            nc.scalar.copy(out=mean[:], in_=mean_turned[:].rearrange("p t g -> p g t"))
            mean_of[0] = mean

        def turn(q):
            turned = turned_pool.tile([P, PAIR, HALVES, P], F32)
            for j, (s, i) in enumerate(teams[q]):
                turn_words(nc, identity, by_graph[s][:, i, :], turned[:, j, :, :])
            kept[("turned", q)] = turned

        def group(q):
            size = len(teams[q])
            grouped = work.tile([P, 2, size, P, PACK], BF16, name="grouped", align_bytes=64, bufs=3 + AHEAD)
            group_words(nc, kept[("turned", q)][:, 0:size, :, :], grouped[:, 0, :, :, :])
            kept[("grouped", q)] = grouped

        def neighbours(q):
            grouped = kept[("grouped", q)][:].rearrange("p x j r t -> p x j (r t)")
            for s in range(BLOCKS):
                mine = [j for j, tile in enumerate(teams[q]) if tile[0] == s]
                if not mine:
                    continue
                mean = mean_of[s][:].rearrange("p g t -> p (g t)").unsqueeze(1)
                nc.vector.scalar_tensor_tensor(
                    out=grouped[:, 1, mine[0] : mine[-1] + 1, :],
                    in0=grouped[:, 0, mine[0] : mine[-1] + 1, :],
                    scalar=-1.0 / OTHERS,
                    in1=mean.to_broadcast([P, len(mine), D]),
                    op0=ALU.mult,
                    op1=ALU.add,
                )

        def quantise(q):
            codes = work.tile([P, 2, len(teams[q]), P], U32, name="codes", align_bytes=64)
            scales = work.tile([P, 2, len(teams[q]), P], U8, name="scales", align_bytes=64)
            nc.vector.quantize_mx(
                out=codes[:].rearrange("p x j r -> p (x j r)").bitcast(FP8X4),
                scales=scales[:].rearrange("p x j r -> p (x j r)"),
                in_=kept[("grouped", q)][:].rearrange("p x j r t -> p (x j r t)"),
            )
            kept[("codes", q)] = (codes, scales)

        def multiply(q):
            codes, scales = kept[("codes", q)]
            banks = []
            for j in range(len(teams[q])):
                acc = acc_pool.tile([P, D], F32)
                nc.tensor.matmul_mx(
                    out=acc[:],
                    lhsT=codes[:, 0, j, :].bitcast(FP8X4),
                    lhsT_scale=scales[:, 0, j, :],
                    rhs=wr_codes[:].bitcast(FP8X4),
                    rhs_scale=wr_scales[:],
                    start=True,
                    stop=False,
                )
                nc.tensor.matmul_mx(
                    out=acc[:],
                    lhsT=codes[:, 1, j, :].bitcast(FP8X4),
                    lhsT_scale=scales[:, 1, j, :],
                    rhs=wl_codes[:].bitcast(FP8X4),
                    rhs_scale=wl_scales[:],
                    start=False,
                    stop=True,
                )
                banks.append(acc)
            kept[("acc", q)] = banks

        def add_bias(q, j):
            if j == 0:
                kept[("c", q)] = work.tile([P, PAIR, D], F32, name="c", bufs=3)
                kept[("row_sum", q)] = stats.tile([P, PAIR], F32, name="row_sum")
            nc.vector.scalar_tensor_tensor(
                out=kept[("c", q)][:, j, :],
                in0=kept[("acc", q)][j][:],
                scalar=1.0,
                in1=bias_rows[:],
                op0=ALU.mult,
                op1=ALU.add,
                accum_out=kept[("row_sum", q)][:, j : j + 1],
            )

        def sum_squares(q, j):
            if j == 0:
                kept[("square_sum", q)] = stats.tile([P, PAIR], F32, name="square_sum")
            squares = work.tile([P, D], BF16, name="squares")
            nc.scalar.activation(
                out=squares[:],
                in_=kept[("c", q)][:, j, :],
                func=ACT.Square,
                bias=kept[("row_sum", q)][:, j : j + 1],
                scale=-float(D),
                accum_out=kept[("square_sum", q)][:, j : j + 1],
            )

        def invert_deviation(q):
            inverse = stats.tile([P, PAIR], F32, name="inverse")
            nc.scalar.activation(
                out=inverse[:, 0 : len(teams[q])],
                in_=kept[("square_sum", q)][:, 0 : len(teams[q])],
                func=ACT.Abs_reciprocal_sqrt,
                bias=eps[:],
                scale=1.0 / D**3,
            )
            kept[("inverse", q)] = inverse

        def admit(q):
            minus_mean = stats.tile([P, PAIR], F32, name="minus_mean_again")
            size = len(teams[q])
            nc.vector.tensor_scalar_mul(
                out=minus_mean[:, 0:size], in0=kept[("row_sum", q)][:, 0:size], scalar1=-1.0 / D
            )
            kept[("minus_mean_again", q)] = minus_mean

        def normalise(q, j):
            if j == 0:
                kept[("normal", q)] = work.tile([P, PAIR, D], F32, name="normal")
            nc.gpsimd.tensor_scalar(
                out=kept[("normal", q)][:, j, :],
                in0=kept[("c", q)][:, j, :],
                scalar1=kept[("minus_mean_again", q)][:, j : j + 1],
                scalar2=kept[("inverse", q)][:, j : j + 1],
                op0=ALU.add,
                op1=ALU.mult,
            )

        def to_features(q):
            normal = kept[("normal", q)]
            banks = []
            for half in range(CHUNKS // 2):
                normal_turned = features_pool.tile([P, 2, PAIR, P], F32)
                for x in range(2):
                    f = 2 * half + x
                    for j in range(len(teams[q])):
                        nc.tensor.transpose(
                            normal_turned[:, x, j, :], normal[:, j, f * P : (f + 1) * P], identity[:]
                        )
                banks.append(normal_turned)
            kept[("normal_turned", q)] = banks

        def two_terms(q, f):
            if f == 0:
                kept[("bent", q)] = work.tile([P, CHUNKS, PAIR, P], F32, name="bent")
                kept[("straight", q)] = work.tile([P, CHUNKS, PAIR, P], F32, name="straight")
            size = len(teams[q])
            turned_chunk = kept[("normal_turned", q)][f // 2][:, f % 2, 0:size, :]
            nc.scalar.activation(
                out=kept[("straight", q)][:, f, 0:size, :],
                in_=turned_chunk,
                func=ACT.Identity,
                bias=line_term[:, CHUNKS + f : CHUNKS + f + 1],
                scale=line_term[:, f : f + 1],
            )
            nc.scalar.activation(
                out=kept[("bent", q)][:, f, 0:size, :],
                in_=turned_chunk,
                func=ACT.Relu,
                bias=relu_term[:, CHUNKS + f : CHUNKS + f + 1],
                scale=relu_term[:, f : f + 1],
            )

        def to_rows(q, j):
            bent, straight = kept[("bent", q)], kept[("straight", q)]
            a_rows = rows_pool.tile([P, D], F32)
            for f in range(CHUNKS):
                nc.tensor.matmul(
                    out=a_rows[:, f * P : (f + 1) * P],
                    lhsT=straight[:, f, j, :],
                    rhs=identity[:],
                    is_transpose=True,
                    start=True,
                    stop=False,
                )
                nc.tensor.matmul(
                    out=a_rows[:, f * P : (f + 1) * P],
                    lhsT=bent[:, f, j, :],
                    rhs=identity[:],
                    is_transpose=True,
                    start=False,
                    stop=True,
                )
            kept[("a_rows", q, j)] = a_rows

        def add_residual(q, j):
            s, i = teams[q][j]
            result = work.tile([P, D], F32, name="result", bufs=4)
            nc.vector.tensor_add(
                out=result[:], in0=kept[("a_rows", q, j)][:], in1=by_graph[s][:, i, :]
            )
            nc.sync.dma_start(out=out[s * P : (s + 1) * P, i, :], in_=result[:])

        def spread_vectors():
            vector_rows_f32 = const.tile([P, P], F32)
            nc.vector.tensor_copy(out=vector_rows_f32[:], in_=vector_rows[:])
            vectors_turned = features_pool.tile([P, P], F32, name="normal_turned")
            nc.tensor.transpose(vectors_turned[:], vector_rows_f32[:], identity[:])
            per_feature = const.tile([P, 2 * CHUNKS], F32)
            nc.vector.tensor_copy(out=per_feature[:], in_=vectors_turned[:, 0 : 2 * CHUNKS])
            relu_term = const.tile([P, 2 * CHUNKS], F32)
            nc.vector.tensor_scalar_mul(out=relu_term[:], in0=per_feature[:], scalar1=1.0 - LEAKY_SLOPE)
            line_term = const.tile([P, 2 * CHUNKS], F32)
            nc.vector.tensor_scalar_mul(out=line_term[:], in0=per_feature[:], scalar1=LEAKY_SLOPE)
            return relu_term, line_term

        def run(stage, q):
            if 0 <= q < count:
                stage(q)

        def run_tiles(stage, q):
            if 0 <= q < count:
                for j in range(len(teams[q])):
                    stage(q, j)

        def run_parts(stage, q, begin, end):
            if 0 <= q < count:
                for f in range(begin, end):
                    stage(q, f)

        row_sums = sums_pool.tile([P, D], F32, name="sums")
        for x in range(WARM_UP):
            nc.tensor.matmul(out=row_sums[:], lhsT=sixteenth[:], rhs=nothing[:], start=True, stop=True)
        turn(0)
        group(0)
        add_nodes(row_sums, range(*RUNS[0]))
        add_nodes(row_sums, range(*RUNS[1]))
        turn(1)
        group(1)
        for x, run_of_nodes in enumerate(RUNS[2:]):
            add_nodes(row_sums, range(*run_of_nodes))
            if x < AHEAD:
                turn(2 + x)
                group(2 + x)
        for x in range(len(RUNS[2:]), AHEAD):
            turn(2 + x)
            group(2 + x)
        mean_rows = means.tile([P, D], F32, name="mean_rows", bufs=1)
        nc.scalar.copy(out=mean_rows[:], in_=row_sums[:])
        wr_grouped = turn_weight(nc, stage, features_pool, identity, wr_rows)
        turn_mean(mean_rows)
        quantise_weight(nc, wr_grouped, wr_codes, wr_scales)
        neighbours(0)
        wl_grouped = turn_weight(nc, stage, features_pool, identity, wl_rows)
        quantise(0)
        neighbours(1)
        quantise_weight(nc, wl_grouped, wl_codes, wl_scales)

        for k in range(HEAD, count + DEPTH):
            if k == 4:
                relu_term, line_term = spread_vectors()
            for s in range(2, BLOCKS):
                since = k - first_team[s - 1] + LOAD_AHEAD
                if 0 <= since < len(RUNS):
                    if s == 2:
                        load_rows(s + 1, *RUNS[since])
                    load_graphs(s, *RUNS[since])
            run_tiles(add_residual, k - 9)
            run_tiles(add_bias, k - 4)
            run_tiles(normalise, k - 6)
            if k > HEAD:
                run(group, k - 1 + AHEAD)
            for s in range(1, BLOCKS):
                if k == first_team[s] - 1:
                    keep_sums(s)
                if k == first_team[s]:
                    keep_rows(s)
            run(to_features, k - 7)
            run_tiles(to_rows, k - 8)
            run(turn, k + AHEAD)
            for s in range(1, BLOCKS):
                since = k - first_team[s] + 1 + CHUNKS
                if 0 <= since < CHUNKS:
                    sum_nodes(s, since)
                if since == CHUNKS:
                    sums_to_rows(s)
                if since == CHUNKS + 1:
                    turn_rows(s)
            run(multiply, k - 3)
            run_tiles(sum_squares, k - 5)
            run_parts(two_terms, k - 7, 0, 1)
            run(invert_deviation, k - 5)
            run_parts(two_terms, k - 7, 1, CHUNKS)
            for s in range(1, BLOCKS):
                if k == first_team[s]:
                    keep_mean(s)
            if k > HEAD:
                run(quantise, k - 2)
            if k > HEAD:
                run(neighbours, k - 1)
            run(admit, k - 5)
